import numpy as np
import ml_dtypes


def mxq(x, axis, fmt="e4m3"):
    dtype, down = {"e4m3": (ml_dtypes.float8_e4m3fn, 7), "e5m2": (ml_dtypes.float8_e5m2, 14)}[fmt]
    v = np.moveaxis(np.asarray(x, np.float32).astype(ml_dtypes.bfloat16).astype(np.float64), axis, -1)
    blocks = v.reshape(v.shape[:-1] + (-1, 32))
    amax = np.abs(blocks).max(-1, keepdims=True)
    byte = np.maximum(np.where(amax > 0, np.frexp(amax)[1] - 1 + 127, 0) - down, 1)
    scale = np.exp2(byte - 127.0)
    codes = (blocks / scale).astype(np.float32).astype(dtype).astype(np.float64)
    return np.moveaxis((codes * scale).reshape(v.shape), -1, axis)


WIDE = False


def mx_kscale(k):
    if not WIDE:
        return np.ones(k)
    levels = np.array([10, -10, 5, -5, 0])
    a = np.random.permutation(np.resize(levels, k // 512 * 4)).reshape(k // 512, 4)
    idx = np.arange(k)
    return np.exp2(a[idx // 512, idx % 128 // 32])


BF16 = ml_dtypes.bfloat16


def bf(x):
    return np.asarray(x, np.float32).astype(BF16)


def f64(x):
    return np.asarray(x).astype(np.float64)


B, LQ, LK, DIN, H = 2, 2048, 1024, 1024, 512
FLOOR = 1e-9


def setup_inputs():
    s = mx_kscale(DIN)
    mass = np.where(np.random.random((B, LQ, 1)) < 0.25, FLOOR, 1.0)
    return {"q": bf(np.random.standard_normal((B, LQ, H)) * 1.5),
            "k": bf(np.random.standard_normal((B, LK, H)) * 1.5),
            "v_ret": bf(np.random.standard_normal((B, LK, DIN)) * s),
            "pi_star": bf(mass * np.exp(1.25 * np.random.standard_normal((B, LQ, LK)))),
            "Wv": bf(np.random.standard_normal((DIN, H)) * 1.5 / np.sqrt(DIN) / s[:, None]),
            "bv": bf(np.random.standard_normal(H) * 0.25),
            "gamma": bf(1.25 + 0.25 * np.random.random(1))}


def reference(q, k, v_ret, pi_star, Wv, bv, gamma):
    wvq = mxq(f64(Wv), 0, "e4m3")
    rows = []
    for b in range(B):
        v = (mxq(f64(v_ret[b]), 1, "e4m3") @ wvq) + f64(bv)
        logits = f64(q[b]) @ f64(k[b]).T / np.sqrt(H)
        z = logits + f64(gamma) * np.log(np.maximum(f64(pi_star[b]), FLOOR))
        e = np.exp(z - z.max(1, keepdims=True))
        rows.append((mxq(e, 1, "e4m3") @ mxq(v, 0, "e4m3")) / e.sum(1, keepdims=True))
    return np.stack(rows)

@@ -1,0 +1,374 @@
+import math
+from contextlib import ExitStack
+
+import concourse.mybir as mybir
+from concourse.masks import make_identity
+
+F32 = mybir.dt.float32
+BF16 = mybir.dt.bfloat16
+U32 = mybir.dt.uint32
+U8 = mybir.dt.uint8
+FP8X4 = mybir.dt.float8_e4m3fn_x4
+ALU = mybir.AluOpType
+ACT = mybir.ActivationFunctionType
+AX = mybir.AxisListType
+
+P = 128
+PACK = 4
+B, LQ, LK, DIN, H = 2, 2048, 1024, 1024, 512
+FLOOR = 1e-9
+FLT_MAX = 3.4028234e38
+FLOPS = 2 * B * (LK * DIN * H + 2 * LQ * LK * H)
+
+NB = LQ // P
+TILES = B * NB
+KEY_TILES = LK // P
+BANK = 512
+
+AHEAD = 4
+EXP_LEAD = 2
+TURN = 4
+OWED = 2
+LAST = 4
+KEYS_TICK = 2
+FEATURES_TICK = 6
+VALUES_TICK = NB - TURN
+FLOOR_TICK = 4
+
+
+def tile_pgwcrossattention_pa_t_kernel(tc, q, k, v_ret, pi_star, Wv, bv, gamma, out):
+    nc = tc.nc
+    inv_sqrt_h = 1.0 / math.sqrt(H)
+    pi_view = pi_star.rearrange("b (t p) k -> p (b t) k", p=P)
+    q_view = q.rearrange("b (t p) h -> p (b t) h", p=P)
+    k_view = k.rearrange("b (t p) h -> p b t h", p=P)
+    vr_view = v_ret.rearrange("b (t p) d -> p b t d", p=P)
+    out_view = out.rearrange("b (t p) h -> p (b t) h", p=P)
+    wv_view = Wv.rearrange("(c p e) h -> p c (e h)", c=4, e=2)
+
+    with ExitStack() as ctx:
+        const = ctx.enter_context(tc.tile_pool(name="const", bufs=1))
+        raw = ctx.enter_context(tc.tile_pool(name="raw", bufs=4))
+        keep = ctx.enter_context(tc.tile_pool(name="keep", bufs=2))
+        work = ctx.enter_context(tc.tile_pool(name="work", bufs=3))
+        psum = ctx.enter_context(tc.psum_pool(name="psum", bufs=2))
+        ctx.enter_context(tc.manual_schedule())
+
+        ident_f32 = const.tile([P, P], F32)
+        make_identity(nc, ident_f32[:])
+        ident_bf16 = const.tile([P, P], BF16)
+        make_identity(nc, ident_bf16[:])
+        gamma_bf = const.tile([P, 1], BF16)
+        bias_bf = const.tile([P, H], BF16)
+        neg_gain = const.tile([P, 1], F32)
+        wv_codes = const.tile([P, 2, H], U32, align_bytes=64)
+        wv_scales = const.tile([P, 2, H], U8, align_bytes=64)
+
+        pi_raw, q_raw, k_raw, vr_raw, wv_raw = {}, {}, {}, {}, {}
+        w, q_t, k_t, z = {}, {}, {}, {}
+        e, e_t, e_grouped, e_codes, e_scales, acc = {}, {}, {}, {}, {}, {}
+        exp_bias, row_sum, row_recip = {}, {}, {}
+        vr_codes, vr_scales, v_grouped, v_codes, v_scales = {}, {}, {}, {}, {}
+
+        def load_pi(c):
+            pi_raw[c] = raw.tile([P, 2, LK], BF16, name="pi_raw")
+            nc.sync.dma_start(out=pi_raw[c][:], in_=pi_view[:, 2 * c : 2 * c + 2, :])
+
+        def load_q(j):
+            q_raw[j] = raw.tile([P, 2, H], BF16, name="q_raw")
+            nc.sync.dma_start(out=q_raw[j][:], in_=q_view[:, 2 * j : 2 * j + 2, :])
+
+        def load_k(b, half):
+            k_raw[b, half] = raw.tile([P, 4, H], BF16, name="k_raw", bufs=2)
+            nc.sync.dma_start(out=k_raw[b, half][:], in_=k_view[:, b, 4 * half : 4 * half + 4, :])
+
+        def load_vr(b, j):
+            vr_raw[b, j] = raw.tile([P, 2, DIN], BF16, name="vr_raw", tag="wide_raw", bufs=6)
+            nc.sync.dma_start(out=vr_raw[b, j][:], in_=vr_view[:, b, 2 * j : 2 * j + 2, :])
+
+        def load_wv(g):
+            wv_raw[g] = raw.tile([P, PACK, H], BF16, name="wv_raw", tag="wide_raw", bufs=6)
+            nc.sync.dma_start(
+                out=wv_raw[g][:].rearrange("p (u e) h -> p u (e h)", u=2), in_=wv_view[:, 2 * g : 2 * g + 2, :]
+            )
+
+        def floor_stage(i):
+            w[i] = keep.tile([P, LK], F32, name="w", bufs=NB + 4)
+            nc.gpsimd.tensor_scalar(
+                out=w[i][:], in0=pi_raw[i // 2][:, i % 2, :], scalar1=FLT_MAX, scalar2=FLOOR, op0=ALU.min, op1=ALU.max
+            )
+
+        def log_stage(i):
+            nc.scalar.activation(out=w[i][:], in_=w[i][:], func=ACT.Ln)
+
+        def transpose_keys(b, j, copy):
+            if j == 0:
+                k_t[b] = keep.tile([P, 2, LK], F32, name="k_t")
+            bank = psum.tile([P, 2, 2, P], F32, name="k_bank", tag="inputs")
+            for u in range(2):
+                for l in range(2):
+                    words = k_raw[b, j // 2][:, 2 * (j % 2) + l, :].bitcast(F32)
+                    nc.tensor.transpose(out=bank[:, u, l, :], in_=words[:, u * P : (u + 1) * P], identity=ident_f32[:])
+            copy(out=k_t[b][:, :, 2 * j * P : (2 * j + 2) * P], in_=bank[:].rearrange("p u l k -> p u (l k)"))
+
+        def transpose_queries(j):
+            bank = psum.tile([P, 2, 2, P], F32, name="q_bank", tag="inputs")
+            for l in range(2):
+                words = q_raw[j][:, l, :].bitcast(F32)
+                for u in range(2):
+                    nc.tensor.transpose(out=bank[:, l, u, :], in_=words[:, u * P : (u + 1) * P], identity=ident_f32[:])
+            q_t[j] = work.tile([P, 2, 2, P], F32, name="q_t")
+            nc.vector.tensor_copy(out=q_t[j][:], in_=bank[:])
+
+        def scores(i, half):
+            keys = k_t[i // NB][:].bitcast(BF16).rearrange("p u (k e) -> p u k e", e=2)
+            z[i, half] = psum.tile([P, BANK], F32, name="z", bufs=3)
+            for u in range(2):
+                rows = q_t[i // 2][:, i % 2, u, :].bitcast(BF16).rearrange("p (q e) -> p q e", e=2)
+                for par in range(2):
+                    nc.tensor.matmul(
+                        out=z[i, half][:],
+                        lhsT=rows[:, :, par],
+                        rhs=keys[:, u, BANK * half : BANK * (half + 1), par],
+                        start=(u == 0 and par == 0),
+                        stop=(u == 1 and par == 1),
+                    )
+
+        def add_prior(i):
+            for half in range(2):
+                cols = slice(BANK * half, BANK * (half + 1))
+                nc.vector.scalar_tensor_tensor(
+                    out=w[i][:, cols], in0=w[i][:, cols], scalar=neg_gain[:, 0:1], in1=z[i, half][:],
+                    op0=ALU.mult, op1=ALU.subtract,
+                )
+            w_min = work.tile([P, 1], F32, name="w_min")
+            nc.vector.tensor_reduce(out=w_min[:], in_=w[i][:], axis=AX.X, op=ALU.min)
+            exp_bias[i] = work.tile([P, 1], F32, name="exp_bias", bufs=8)
+            nc.vector.tensor_scalar(out=exp_bias[i][:], in0=w_min[:], scalar1=inv_sqrt_h, scalar2=None, op0=ALU.mult)
+
+        def exp_stage(i):
+            e[i] = work.tile([P, LK], BF16, name="e", bufs=EXP_LEAD + 3)
+            row_sum[i] = work.tile([P, 1], F32, name="row_sum", bufs=8)
+            nc.scalar.activation(
+                out=e[i][:], in_=w[i][:], func=ACT.Exp, bias=exp_bias[i][:, 0:1], scale=-inv_sqrt_h,
+                accum_out=row_sum[i][:, 0:1],
+            )
+
+        def transpose_probs(i):
+            e_t[i] = psum.tile([P, KEY_TILES, P], BF16, name="e_t", bufs=1)
+            for kt in range(KEY_TILES):
+                nc.tensor.transpose(out=e_t[i][:, kt, :], in_=e[i][:, kt * P : (kt + 1) * P], identity=ident_bf16[:])
+
+        def regroup_probs(i, copy):
+            e_grouped[i] = work.tile([P, 2, P, PACK], BF16, name="e_grouped", align_bytes=64)
+            copy(out=e_grouped[i][:], in_=e_t[i][:].rearrange("p (c t) r -> p c r t", t=PACK))
+
+        def quantise_probs(i):
+            e_codes[i] = work.tile([P, 2 * P], U32, name="e_codes", align_bytes=64)
+            e_scales[i] = work.tile([P, 2 * P], U8, name="e_scales", align_bytes=64)
+            nc.vector.quantize_mx(
+                out=e_codes[i][:].bitcast(FP8X4), scales=e_scales[i][:],
+                in_=e_grouped[i][:].rearrange("p c r t -> p (c r t)"),
+            )
+            row_recip[i] = work.tile([P, 1], F32, name="row_recip", bufs=4)
+            nc.vector.reciprocal(out=row_recip[i][:], in_=row_sum[i][:])
+
+        def weighted_values(i):
+            acc[i] = psum.tile([P, H], F32, name="acc", tag="mx")
+            for c in range(2):
+                nc.tensor.matmul_mx(
+                    out=acc[i][:],
+                    lhsT=e_codes[i][:, c * P : (c + 1) * P].bitcast(FP8X4),
+                    lhsT_scale=e_scales[i][:, c * P : (c + 1) * P],
+                    rhs=v_codes[i // NB][:, c, :].bitcast(FP8X4),
+                    rhs_scale=v_scales[i // NB][:, c, :],
+                    start=(c == 0),
+                    stop=(c == 1),
+                )
+
+        def normalise_and_store(i, on_vector):
+            o = work.tile([P, H], F32, name="o", bufs=2)
+            if on_vector:
+                nc.vector.tensor_scalar(out=o[:], in0=acc[i][:], scalar1=row_recip[i][:, 0:1], scalar2=None, op0=ALU.mult)
+            else:
+                nc.scalar.activation(out=o[:], in_=acc[i][:], func=ACT.Copy, scale=row_recip[i][:, 0:1])
+            nc.sync.dma_start(out=out_view[:, i, :], in_=o[:])
+
+        def quantise_weights(g):
+            grouped = work.tile([P, H, PACK], BF16, name="wv_grouped", tag="grouped", align_bytes=64)
+            nc.vector.tensor_copy(out=grouped[:], in_=wv_raw[g][:].rearrange("p t h -> p h t"))
+            nc.vector.quantize_mx(
+                out=wv_codes[:, g, :].bitcast(FP8X4), scales=wv_scales[:, g, :], in_=grouped[:].rearrange("p h t -> p (h t)")
+            )
+
+        def transpose_features(b, j, copies):
+            if j == 0:
+                vr_codes[b] = keep.tile([P, KEY_TILES, 2, P], U32, name="vr_codes", bufs=1, align_bytes=64)
+                vr_scales[b] = keep.tile([P, KEY_TILES, 2, P], U8, name="vr_scales", bufs=1, align_bytes=64)
+            grouped = work.tile([P, 2, 2, P, PACK], BF16, name="vr_grouped", tag="grouped", align_bytes=64)
+            for l in range(2):
+                bank = psum.tile([P, 2, 2, P], F32, name="vr_bank", tag="inputs")
+                words = vr_raw[b, j][:, l, :].bitcast(F32)
+                for g in range(2):
+                    for u in range(2):
+                        c = 2 * g + u
+                        nc.tensor.transpose(out=bank[:, g, u, :], in_=words[:, c * P : (c + 1) * P], identity=ident_f32[:])
+                copies[l](out=grouped[:].bitcast(F32)[:, l], in_=bank[:].rearrange("p g u k -> p g k u"))
+            nc.vector.quantize_mx(
+                out=vr_codes[b][:, 2 * j : 2 * j + 2].rearrange("p l g k -> p (l g k)").bitcast(FP8X4),
+                scales=vr_scales[b][:, 2 * j : 2 * j + 2].rearrange("p l g k -> p (l g k)"),
+                in_=grouped[:].rearrange("p l g k t -> p (l g k t)"),
+            )
+
+        def project_values(b, n):
+            c, hc = n // 4, n % 4
+            cols = slice(hc * P, (hc + 1) * P)
+            if n == 0:
+                v_codes[b] = keep.tile([P, 2, H], U32, name="v_codes", align_bytes=64)
+                v_scales[b] = keep.tile([P, 2, H], U8, name="v_scales", align_bytes=64)
+            if hc == 0:
+                v_grouped[b] = work.tile([P, H, PACK], BF16, name="v_grouped", tag="grouped", align_bytes=64)
+            bank = psum.tile([P, PACK, P], F32, name="v_bank", tag="mx")
+            for t in range(PACK):
+                for g in range(2):
+                    nc.tensor.matmul_mx(
+                        out=bank[:, t, :],
+                        lhsT=vr_codes[b][:, PACK * c + t, g, :].bitcast(FP8X4),
+                        lhsT_scale=vr_scales[b][:, PACK * c + t, g, :],
+                        rhs=wv_codes[:, g, cols].bitcast(FP8X4),
+                        rhs_scale=wv_scales[:, g, cols],
+                        start=(g == 0),
+                        stop=(g == 1),
+                    )
+            nc.vector.tensor_tensor(
+                out=v_grouped[b][:, cols, :],
+                in0=bank[:].rearrange("p t h -> p h t"),
+                in1=bias_bf[:, cols].unsqueeze(2).to_broadcast([P, P, PACK]),
+                op=ALU.add,
+            )
+            if hc == 3:
+                nc.vector.quantize_mx(
+                    out=v_codes[b][:, c, :].bitcast(FP8X4), scales=v_scales[b][:, c, :],
+                    in_=v_grouped[b][:].rearrange("p h t -> p (h t)"),
+                )
+
+        def logs(first, count):
+            for i in range(first, first + count):
+                floor_stage(i)
+                log_stage(i)
+
+        def first_scores(i):
+            scores(i, 0)
+            scores(i, 1)
+            add_prior(i)
+
+        warm = const.tile([P, 1], F32)
+        nc.vector.memset(warm[:], 1.0)
+        nc.scalar.activation(out=warm[:], in_=warm[:], func=ACT.Ln)
+        load_pi(0)
+        load_k(0, 0)
+        load_pi(1)
+        load_k(0, 1)
+        load_q(0)
+        nc.sync.dma_start(out=gamma_bf[:], in_=gamma.partition_broadcast(P))
+        load_pi(2)
+        load_wv(0)
+        load_pi(3)
+        load_wv(1)
+        load_q(1)
+        logs(0, 4)
+        for j in range(4):
+            transpose_keys(0, j, nc.vector.tensor_copy)
+        nc.vector.tensor_scalar(out=neg_gain[:], in0=gamma_bf[:], scalar1=-math.sqrt(H), scalar2=None, op0=ALU.mult)
+        load_pi(4)
+        load_vr(0, 0)
+        load_pi(5)
+        load_vr(0, 1)
+        nc.sync.dma_start(out=bias_bf[:], in_=bv.partition_broadcast(P))
+        logs(4, 4)
+        load_pi(6)
+        load_vr(0, 2)
+        load_pi(7)
+        load_vr(0, 3)
+        load_q(2)
+        load_q(3)
+        transpose_queries(0)
+        first_scores(0)
+        first_scores(1)
+        transpose_queries(1)
+        quantise_weights(0)
+        logs(8, 1)
+        for j in range(4):
+            transpose_features(0, j, (nc.scalar.copy, nc.scalar.copy))
+            if j < 2:
+                first_scores(2 + j)
+            if j == 0:
+                quantise_weights(1)
+            logs(9 + 2 * j, min(2, NB - 9 - 2 * j))
+        transpose_queries(AHEAD // 2)
+        for n in range(8):
+            project_values(0, n)
+        for i in range(EXP_LEAD):
+            exp_stage(i)
+        transpose_probs(0)
+
+        def tile_of(t):
+            if t < 0 or NB - OWED <= t < NB:
+                return -1
+            i = t if t < NB else t - OWED
+            return i if i < TILES else -1
+
+        def beside_logs(i):
+            return NB - TURN <= i < NB - OWED or i >= TILES - LAST
+
+        for t in range(TILES + OWED + 1):
+            tt = t % NB
+            nb = t // NB + 1
+            turning = nb < B and tt >= NB - TURN
+            cur, prev, following = tile_of(t), tile_of(t - 1), tile_of(t + 1)
+            ahead = t + AHEAD
+            if nb < B:
+                if tt < 2:
+                    load_k(nb, tt)
+                if 2 <= tt < 6:
+                    load_vr(nb, tt - 2)
+                if 1 <= tt < 1 + NB // 2:
+                    load_pi(nb * NB // 2 + tt - 1)
+            if ahead % 2 == 0 and 2 * AHEAD <= ahead + AHEAD < TILES:
+                load_q((ahead + AHEAD) // 2)
+            if nb < B and FLOOR_TICK <= tt < FLOOR_TICK + NB // 2:
+                floor_stage(nb * NB + 2 * (tt - FLOOR_TICK))
+                floor_stage(nb * NB + 2 * (tt - FLOOR_TICK) + 1)
+            if cur >= 0:
+                regroup_probs(cur, nc.vector.tensor_copy if beside_logs(cur) else nc.scalar.copy)
+            if nb < B and KEYS_TICK <= tt < KEYS_TICK + 4:
+                transpose_keys(nb, tt - KEYS_TICK, nc.scalar.copy)
+            if (ahead + 1) % 2 == 0 and ahead + 1 < TILES:
+                transpose_queries((ahead + 1) // 2)
+            if ahead < TILES:
+                scores(ahead, 0)
+            if AHEAD <= ahead - 1 < TILES:
+                add_prior(ahead - 1)
+            if cur >= 0:
+                quantise_probs(cur)
+            if nb < B and VALUES_TICK <= tt:
+                project_values(nb, 2 * (tt - VALUES_TICK))
+                project_values(nb, 2 * (tt - VALUES_TICK) + 1)
+            if prev >= 0:
+                weighted_values(prev)
+            if ahead < TILES:
+                scores(ahead, 1)
+            if nb < B and FEATURES_TICK <= tt < FEATURES_TICK + 4:
+                transpose_features(nb, tt - FEATURES_TICK, (nc.scalar.copy, nc.vector.tensor_copy))
+            if turning:
+                for n in range(NB // TURN):
+                    log_stage(nb * NB + (tt - (NB - TURN)) * (NB // TURN) + n)
+                if tt == NB - 1:
+                    for i in range(nb * NB - OWED, nb * NB):
+                        exp_stage(i)
+            elif cur >= 0 and cur + EXP_LEAD < TILES:
+                exp_stage(cur + EXP_LEAD)
+            if following >= 0:
+                transpose_probs(following)
+            if prev >= 0:
+                normalise_and_store(prev, beside_logs(prev))

@@ -24,6 +24,7 @@ NB = LQ // P
 TILES = B * NB
 KEY_TILES = LK // P
 BANK = 512
+GAMMA_COLS = 32
 
 AHEAD = 4
 EXP_LEAD = 2
@@ -33,17 +34,17 @@ LAST = 4
 KEYS_TICK = 2
 FEATURES_TICK = 6
 VALUES_TICK = NB - TURN
-FLOOR_TICK = 4
+SPARE = 4
 
 
 def tile_pgwcrossattention_pa_t_kernel(tc, q, k, v_ret, pi_star, Wv, bv, gamma, out):
     nc = tc.nc
     inv_sqrt_h = 1.0 / math.sqrt(H)
-    pi_view = pi_star.rearrange("b (t p) k -> p (b t) k", p=P)
-    q_view = q.rearrange("b (t p) h -> p (b t) h", p=P)
+    pi_view = pi_star.rearrange("b (j p l) k -> p (b j) l k", p=P, l=2)
+    q_view = q.rearrange("b (j p l) h -> p (b j) l h", p=P, l=2)
+    out_view = out.rearrange("b (j p l) h -> p (b j) l h", p=P, l=2)
     k_view = k.rearrange("b (t p) h -> p b t h", p=P)
     vr_view = v_ret.rearrange("b (t p) d -> p b t d", p=P)
-    out_view = out.rearrange("b (t p) h -> p (b t) h", p=P)
     wv_view = Wv.rearrange("(c p e) h -> p c (e h)", c=4, e=2)
 
     with ExitStack() as ctx:
@@ -58,7 +59,6 @@ def tile_pgwcrossattention_pa_t_kernel(tc, q, k, v_ret, pi_star, Wv, bv, gamma, 
         make_identity(nc, ident_f32[:])
         ident_bf16 = const.tile([P, P], BF16)
         make_identity(nc, ident_bf16[:])
-        gamma_bf = const.tile([P, 1], BF16)
         bias_bf = const.tile([P, H], BF16)
         neg_gain = const.tile([P, 1], F32)
         wv_codes = const.tile([P, 2, H], U32, align_bytes=64)
@@ -68,15 +68,15 @@ def tile_pgwcrossattention_pa_t_kernel(tc, q, k, v_ret, pi_star, Wv, bv, gamma, 
         w, q_t, k_t, z = {}, {}, {}, {}
         e, e_t, e_grouped, e_codes, e_scales, acc = {}, {}, {}, {}, {}, {}
         exp_bias, row_sum, row_recip = {}, {}, {}
-        vr_codes, vr_scales, v_grouped, v_codes, v_scales = {}, {}, {}, {}, {}
+        vr_grouped, vr_codes, vr_scales, v_grouped, v_codes, v_scales = {}, {}, {}, {}, {}, {}
 
         def load_pi(c):
             pi_raw[c] = raw.tile([P, 2, LK], BF16, name="pi_raw")
-            nc.sync.dma_start(out=pi_raw[c][:], in_=pi_view[:, 2 * c : 2 * c + 2, :])
+            nc.sync.dma_start(out=pi_raw[c][:], in_=pi_view[:, c])
 
         def load_q(j):
             q_raw[j] = raw.tile([P, 2, H], BF16, name="q_raw")
-            nc.sync.dma_start(out=q_raw[j][:], in_=q_view[:, 2 * j : 2 * j + 2, :])
+            nc.sync.dma_start(out=q_raw[j][:], in_=q_view[:, j])
 
         def load_k(b, half):
             k_raw[b, half] = raw.tile([P, 4, H], BF16, name="k_raw", bufs=2)
@@ -92,9 +92,9 @@ def tile_pgwcrossattention_pa_t_kernel(tc, q, k, v_ret, pi_star, Wv, bv, gamma, 
                 out=wv_raw[g][:].rearrange("p (u e) h -> p u (e h)", u=2), in_=wv_view[:, 2 * g : 2 * g + 2, :]
             )
 
-        def floor_stage(i):
-            w[i] = keep.tile([P, LK], F32, name="w", bufs=NB + 4)
-            nc.gpsimd.tensor_scalar(
+        def floor_stage(i, engine):
+            w[i] = keep.tile([P, LK], F32, name="w", bufs=NB + SPARE)
+            engine.tensor_scalar(
                 out=w[i][:], in0=pi_raw[i // 2][:, i % 2, :], scalar1=FLT_MAX, scalar2=FLOOR, op0=ALU.min, op1=ALU.max
             )
 
@@ -155,7 +155,10 @@ def tile_pgwcrossattention_pa_t_kernel(tc, q, k, v_ret, pi_star, Wv, bv, gamma, 
             )
 
         def transpose_probs(i):
-            e_t[i] = psum.tile([P, KEY_TILES, P], BF16, name="e_t", bufs=1)
+            if i >= TILES - LAST:
+                e_t[i] = psum.tile([P, KEY_TILES, P], BF16, name="e_t_last", tag="z", bufs=3)
+            else:
+                e_t[i] = psum.tile([P, KEY_TILES, P], BF16, name="e_t", bufs=1)
             for kt in range(KEY_TILES):
                 nc.tensor.transpose(out=e_t[i][:, kt, :], in_=e[i][:, kt * P : (kt + 1) * P], identity=ident_bf16[:])
 
@@ -187,12 +190,12 @@ def tile_pgwcrossattention_pa_t_kernel(tc, q, k, v_ret, pi_star, Wv, bv, gamma, 
                 )
 
         def normalise_and_store(i, on_vector):
-            o = work.tile([P, H], F32, name="o", bufs=2)
+            o = work.tile([P, H], F32, name="o", bufs=4)
             if on_vector:
                 nc.vector.tensor_scalar(out=o[:], in0=acc[i][:], scalar1=row_recip[i][:, 0:1], scalar2=None, op0=ALU.mult)
             else:
                 nc.scalar.activation(out=o[:], in_=acc[i][:], func=ACT.Copy, scale=row_recip[i][:, 0:1])
-            nc.sync.dma_start(out=out_view[:, i, :], in_=o[:])
+            nc.sync.dma_start(out=out_view[:, i // 2, i % 2, :], in_=o[:])
 
         def quantise_weights(g):
             grouped = work.tile([P, H, PACK], BF16, name="wv_grouped", tag="grouped", align_bytes=64)
@@ -205,7 +208,7 @@ def tile_pgwcrossattention_pa_t_kernel(tc, q, k, v_ret, pi_star, Wv, bv, gamma, 
             if j == 0:
                 vr_codes[b] = keep.tile([P, KEY_TILES, 2, P], U32, name="vr_codes", bufs=1, align_bytes=64)
                 vr_scales[b] = keep.tile([P, KEY_TILES, 2, P], U8, name="vr_scales", bufs=1, align_bytes=64)
-            grouped = work.tile([P, 2, 2, P, PACK], BF16, name="vr_grouped", tag="grouped", align_bytes=64)
+            vr_grouped[b, j] = work.tile([P, 2, 2, P, PACK], BF16, name="vr_grouped", tag="grouped", align_bytes=64)
             for l in range(2):
                 bank = psum.tile([P, 2, 2, P], F32, name="vr_bank", tag="inputs")
                 words = vr_raw[b, j][:, l, :].bitcast(F32)
@@ -213,11 +216,13 @@ def tile_pgwcrossattention_pa_t_kernel(tc, q, k, v_ret, pi_star, Wv, bv, gamma, 
                     for u in range(2):
                         c = 2 * g + u
                         nc.tensor.transpose(out=bank[:, g, u, :], in_=words[:, c * P : (c + 1) * P], identity=ident_f32[:])
-                copies[l](out=grouped[:].bitcast(F32)[:, l], in_=bank[:].rearrange("p g u k -> p g k u"))
+                copies[l](out=vr_grouped[b, j][:].bitcast(F32)[:, l], in_=bank[:].rearrange("p g u k -> p g k u"))
+
+        def quantise_features(b, j):
             nc.vector.quantize_mx(
                 out=vr_codes[b][:, 2 * j : 2 * j + 2].rearrange("p l g k -> p (l g k)").bitcast(FP8X4),
                 scales=vr_scales[b][:, 2 * j : 2 * j + 2].rearrange("p l g k -> p (l g k)"),
-                in_=grouped[:].rearrange("p l g k t -> p (l g k t)"),
+                in_=vr_grouped[b, j][:].rearrange("p l g k t -> p (l g k t)"),
             )
 
         def project_values(b, n):
@@ -254,7 +259,7 @@ def tile_pgwcrossattention_pa_t_kernel(tc, q, k, v_ret, pi_star, Wv, bv, gamma, 
 
         def logs(first, count):
             for i in range(first, first + count):
-                floor_stage(i)
+                floor_stage(i, nc.gpsimd if i % 2 == 0 else nc.vector)
                 log_stage(i)
 
         def first_scores(i):
@@ -262,6 +267,12 @@ def tile_pgwcrossattention_pa_t_kernel(tc, q, k, v_ret, pi_star, Wv, bv, gamma, 
             scores(i, 1)
             add_prior(i)
 
+        ones = const.tile([P, P], BF16)
+        nc.vector.memset(ones[:], 1.0)
+        rows = const.tile([P, H + GAMMA_COLS], BF16)
+        nc.vector.memset(rows[:], 0.0)
+        nc.scalar.dma_start(out=rows[0:1, 0:H], in_=bv.unsqueeze(0))
+        nc.scalar.dma_start(out=rows[0:1, H : H + 1], in_=gamma.unsqueeze(0))
         warm = const.tile([P, 1], F32)
         nc.vector.memset(warm[:], 1.0)
         nc.scalar.activation(out=warm[:], in_=warm[:], func=ACT.Ln)
@@ -270,41 +281,59 @@ def tile_pgwcrossattention_pa_t_kernel(tc, q, k, v_ret, pi_star, Wv, bv, gamma, 
         load_pi(1)
         load_k(0, 1)
         load_q(0)
-        nc.sync.dma_start(out=gamma_bf[:], in_=gamma.partition_broadcast(P))
         load_pi(2)
         load_wv(0)
         load_pi(3)
         load_wv(1)
         load_q(1)
-        logs(0, 4)
-        for j in range(4):
-            transpose_keys(0, j, nc.vector.tensor_copy)
-        nc.vector.tensor_scalar(out=neg_gain[:], in0=gamma_bf[:], scalar1=-math.sqrt(H), scalar2=None, op0=ALU.mult)
+        bias_bank = psum.tile([P, H], F32, name="bias_bank", tag="inputs")
+        nc.tensor.matmul(out=bias_bank[:], lhsT=ones[:], rhs=rows[:, 0:H], start=True, stop=True)
+        nc.vector.tensor_copy(out=bias_bf[:], in_=bias_bank[:])
+        gamma_bank = psum.tile([P, GAMMA_COLS], F32, name="gamma_bank", tag="inputs")
+        nc.tensor.matmul(out=gamma_bank[:], lhsT=ones[:], rhs=rows[:, H : H + GAMMA_COLS], start=True, stop=True)
+        nc.vector.tensor_scalar(out=neg_gain[:], in0=gamma_bank[:, 0:1], scalar1=-math.sqrt(H), scalar2=None, op0=ALU.mult)
+        transpose_keys(0, 0, nc.scalar.copy)
+        transpose_keys(0, 1, nc.scalar.copy)
+        logs(0, 2)
         load_pi(4)
         load_vr(0, 0)
+        transpose_keys(0, 2, nc.scalar.copy)
+        transpose_keys(0, 3, nc.scalar.copy)
+        logs(2, 2)
         load_pi(5)
         load_vr(0, 1)
-        nc.sync.dma_start(out=bias_bf[:], in_=bv.partition_broadcast(P))
-        logs(4, 4)
+        logs(4, 2)
         load_pi(6)
         load_vr(0, 2)
+        transpose_queries(0)
+        logs(6, 2)
         load_pi(7)
         load_vr(0, 3)
         load_q(2)
         load_q(3)
-        transpose_queries(0)
         first_scores(0)
+        logs(8, 2)
         first_scores(1)
         transpose_queries(1)
+        transpose_features(0, 0, (nc.scalar.copy, nc.scalar.copy))
+        logs(10, 2)
         quantise_weights(0)
-        logs(8, 1)
-        for j in range(4):
-            transpose_features(0, j, (nc.scalar.copy, nc.scalar.copy))
-            if j < 2:
-                first_scores(2 + j)
-            if j == 0:
-                quantise_weights(1)
-            logs(9 + 2 * j, min(2, NB - 9 - 2 * j))
+        transpose_features(0, 1, (nc.scalar.copy, nc.scalar.copy))
+        logs(12, 2)
+        quantise_features(0, 0)
+        first_scores(2)
+        transpose_features(0, 2, (nc.scalar.copy, nc.scalar.copy))
+        logs(14, 2)
+        for c in range(NB // 2, NB // 2 + 3):
+            load_pi(c)
+        for i in range(NB, NB + SPARE):
+            floor_stage(i, nc.gpsimd)
+        quantise_features(0, 1)
+        quantise_weights(1)
+        first_scores(3)
+        transpose_features(0, 3, (nc.scalar.copy, nc.scalar.copy))
+        quantise_features(0, 2)
+        quantise_features(0, 3)
         transpose_queries(AHEAD // 2)
         for n in range(8):
             project_values(0, n)
@@ -319,7 +348,10 @@ def tile_pgwcrossattention_pa_t_kernel(tc, q, k, v_ret, pi_star, Wv, bv, gamma, 
             return i if i < TILES else -1
 
         def beside_logs(i):
-            return NB - TURN <= i < NB - OWED or i >= TILES - LAST
+            return NB - TURN <= i < NB - OWED
+
+        def among_last(i):
+            return i >= TILES - LAST
 
         for t in range(TILES + OWED + 1):
             tt = t % NB
@@ -332,15 +364,14 @@ def tile_pgwcrossattention_pa_t_kernel(tc, q, k, v_ret, pi_star, Wv, bv, gamma, 
                     load_k(nb, tt)
                 if 2 <= tt < 6:
                     load_vr(nb, tt - 2)
-                if 1 <= tt < 1 + NB // 2:
-                    load_pi(nb * NB // 2 + tt - 1)
+                if tt % 2 == 0 and tt < NB - SPARE - 2:
+                    load_pi((nb * NB + SPARE + tt + 2) // 2)
             if ahead % 2 == 0 and 2 * AHEAD <= ahead + AHEAD < TILES:
                 load_q((ahead + AHEAD) // 2)
-            if nb < B and FLOOR_TICK <= tt < FLOOR_TICK + NB // 2:
-                floor_stage(nb * NB + 2 * (tt - FLOOR_TICK))
-                floor_stage(nb * NB + 2 * (tt - FLOOR_TICK) + 1)
+            if nb < B and tt < NB - SPARE:
+                floor_stage(nb * NB + SPARE + tt, nc.gpsimd)
             if cur >= 0:
-                regroup_probs(cur, nc.vector.tensor_copy if beside_logs(cur) else nc.scalar.copy)
+                regroup_probs(cur, nc.vector.tensor_copy if beside_logs(cur) or among_last(cur) else nc.scalar.copy)
             if nb < B and KEYS_TICK <= tt < KEYS_TICK + 4:
                 transpose_keys(nb, tt - KEYS_TICK, nc.scalar.copy)
             if (ahead + 1) % 2 == 0 and ahead + 1 < TILES:
@@ -360,6 +391,7 @@ def tile_pgwcrossattention_pa_t_kernel(tc, q, k, v_ret, pi_star, Wv, bv, gamma, 
                 scores(ahead, 1)
             if nb < B and FEATURES_TICK <= tt < FEATURES_TICK + 4:
                 transpose_features(nb, tt - FEATURES_TICK, (nc.scalar.copy, nc.vector.tensor_copy))
+                quantise_features(nb, tt - FEATURES_TICK)
             if turning:
                 for n in range(NB // TURN):
                     log_stage(nb * NB + (tt - (NB - TURN)) * (NB // TURN) + n)

@@ -24,7 +24,6 @@ NB = LQ // P
 TILES = B * NB
 KEY_TILES = LK // P
 BANK = 512
-GAMMA_COLS = 32
 
 AHEAD = 4
 EXP_LEAD = 2
@@ -32,20 +31,20 @@ TURN = 4
 OWED = 2
 LAST = 4
 KEYS_TICK = 2
-FEATURES_TICK = 6
+FEATURES_TICK = 3
 VALUES_TICK = NB - TURN
-SPARE = 4
+FLOOR_TICK = 4
 
 
 def tile_pgwcrossattention_pa_t_kernel(tc, q, k, v_ret, pi_star, Wv, bv, gamma, out):
     nc = tc.nc
     inv_sqrt_h = 1.0 / math.sqrt(H)
-    pi_view = pi_star.rearrange("b (j p l) k -> p (b j) l k", p=P, l=2)
-    q_view = q.rearrange("b (j p l) h -> p (b j) l h", p=P, l=2)
-    out_view = out.rearrange("b (j p l) h -> p (b j) l h", p=P, l=2)
-    k_view = k.rearrange("b (t p) h -> p b t h", p=P)
-    vr_view = v_ret.rearrange("b (t p) d -> p b t d", p=P)
-    wv_view = Wv.rearrange("(c p e) h -> p c (e h)", c=4, e=2)
+    pi_view = pi_star.rearrange("b (n p) k -> p (b n) k", p=P)
+    q_view = q.rearrange("b (n p) h -> p (b n) h", p=P)
+    k_view = k.rearrange("b (n p) h -> p b n h", p=P)
+    vr_view = v_ret.rearrange("b (n p) d -> p b n d", p=P)
+    out_view = out.rearrange("b (n p) h -> p (b n) h", p=P)
+    wv_view = Wv.rearrange("(a p y) h -> p a (y h)", a=4, y=2)
 
     with ExitStack() as ctx:
         const = ctx.enter_context(tc.tile_pool(name="const", bufs=1))
@@ -59,6 +58,7 @@ def tile_pgwcrossattention_pa_t_kernel(tc, q, k, v_ret, pi_star, Wv, bv, gamma, 
         make_identity(nc, ident_f32[:])
         ident_bf16 = const.tile([P, P], BF16)
         make_identity(nc, ident_bf16[:])
+        gamma_bf = const.tile([P, 1], BF16)
         bias_bf = const.tile([P, H], BF16)
         neg_gain = const.tile([P, 1], F32)
         wv_codes = const.tile([P, 2, H], U32, align_bytes=64)
@@ -68,15 +68,15 @@ def tile_pgwcrossattention_pa_t_kernel(tc, q, k, v_ret, pi_star, Wv, bv, gamma, 
         w, q_t, k_t, z = {}, {}, {}, {}
         e, e_t, e_grouped, e_codes, e_scales, acc = {}, {}, {}, {}, {}, {}
         exp_bias, row_sum, row_recip = {}, {}, {}
-        vr_grouped, vr_codes, vr_scales, v_grouped, v_codes, v_scales = {}, {}, {}, {}, {}, {}
+        vr_codes, vr_scales, v_grouped, v_codes, v_scales = {}, {}, {}, {}, {}
 
-        def load_pi(c):
-            pi_raw[c] = raw.tile([P, 2, LK], BF16, name="pi_raw")
-            nc.sync.dma_start(out=pi_raw[c][:], in_=pi_view[:, c])
+        def load_pi(j):
+            pi_raw[j] = raw.tile([P, 2, LK], BF16, name="pi_raw")
+            nc.sync.dma_start(out=pi_raw[j][:], in_=pi_view[:, 2 * j : 2 * j + 2, :])
 
         def load_q(j):
             q_raw[j] = raw.tile([P, 2, H], BF16, name="q_raw")
-            nc.sync.dma_start(out=q_raw[j][:], in_=q_view[:, j])
+            nc.sync.dma_start(out=q_raw[j][:], in_=q_view[:, 2 * j : 2 * j + 2, :])
 
         def load_k(b, half):
             k_raw[b, half] = raw.tile([P, 4, H], BF16, name="k_raw", bufs=2)
@@ -89,12 +89,12 @@ def tile_pgwcrossattention_pa_t_kernel(tc, q, k, v_ret, pi_star, Wv, bv, gamma, 
         def load_wv(g):
             wv_raw[g] = raw.tile([P, PACK, H], BF16, name="wv_raw", tag="wide_raw", bufs=6)
             nc.sync.dma_start(
-                out=wv_raw[g][:].rearrange("p (u e) h -> p u (e h)", u=2), in_=wv_view[:, 2 * g : 2 * g + 2, :]
+                out=wv_raw[g][:].rearrange("p (u y) h -> p u (y h)", u=2), in_=wv_view[:, 2 * g : 2 * g + 2, :]
             )
 
-        def floor_stage(i, engine):
-            w[i] = keep.tile([P, LK], F32, name="w", bufs=NB + SPARE)
-            engine.tensor_scalar(
+        def floor_stage(i):
+            w[i] = keep.tile([P, LK], F32, name="w", bufs=NB + 4)
+            nc.gpsimd.tensor_scalar(
                 out=w[i][:], in0=pi_raw[i // 2][:, i % 2, :], scalar1=FLT_MAX, scalar2=FLOOR, op0=ALU.min, op1=ALU.max
             )
 
@@ -121,17 +121,17 @@ def tile_pgwcrossattention_pa_t_kernel(tc, q, k, v_ret, pi_star, Wv, bv, gamma, 
             nc.vector.tensor_copy(out=q_t[j][:], in_=bank[:])
 
         def scores(i, half):
-            keys = k_t[i // NB][:].bitcast(BF16).rearrange("p u (k e) -> p u k e", e=2)
+            keys = k_t[i // NB][:].bitcast(BF16).rearrange("p u (k y) -> p u k y", y=2)
             z[i, half] = psum.tile([P, BANK], F32, name="z", bufs=3)
             for u in range(2):
-                rows = q_t[i // 2][:, i % 2, u, :].bitcast(BF16).rearrange("p (q e) -> p q e", e=2)
-                for par in range(2):
+                rows = q_t[i // 2][:, i % 2, u, :].bitcast(BF16).rearrange("p (r y) -> p r y", y=2)
+                for y in range(2):
                     nc.tensor.matmul(
                         out=z[i, half][:],
-                        lhsT=rows[:, :, par],
-                        rhs=keys[:, u, BANK * half : BANK * (half + 1), par],
-                        start=(u == 0 and par == 0),
-                        stop=(u == 1 and par == 1),
+                        lhsT=rows[:, :, y],
+                        rhs=keys[:, u, BANK * half : BANK * (half + 1), y],
+                        start=(u == 0 and y == 0),
+                        stop=(u == 1 and y == 1),
                     )
 
         def add_prior(i):
@@ -195,7 +195,7 @@ def tile_pgwcrossattention_pa_t_kernel(tc, q, k, v_ret, pi_star, Wv, bv, gamma, 
                 nc.vector.tensor_scalar(out=o[:], in0=acc[i][:], scalar1=row_recip[i][:, 0:1], scalar2=None, op0=ALU.mult)
             else:
                 nc.scalar.activation(out=o[:], in_=acc[i][:], func=ACT.Copy, scale=row_recip[i][:, 0:1])
-            nc.sync.dma_start(out=out_view[:, i // 2, i % 2, :], in_=o[:])
+            nc.sync.dma_start(out=out_view[:, i, :], in_=o[:])
 
         def quantise_weights(g):
             grouped = work.tile([P, H, PACK], BF16, name="wv_grouped", tag="grouped", align_bytes=64)
@@ -208,21 +208,19 @@ def tile_pgwcrossattention_pa_t_kernel(tc, q, k, v_ret, pi_star, Wv, bv, gamma, 
             if j == 0:
                 vr_codes[b] = keep.tile([P, KEY_TILES, 2, P], U32, name="vr_codes", bufs=1, align_bytes=64)
                 vr_scales[b] = keep.tile([P, KEY_TILES, 2, P], U8, name="vr_scales", bufs=1, align_bytes=64)
-            vr_grouped[b, j] = work.tile([P, 2, 2, P, PACK], BF16, name="vr_grouped", tag="grouped", align_bytes=64)
+            grouped = work.tile([P, 2, 2, P, PACK], BF16, name="vr_grouped", tag="grouped", align_bytes=64)
             for l in range(2):
                 bank = psum.tile([P, 2, 2, P], F32, name="vr_bank", tag="inputs")
                 words = vr_raw[b, j][:, l, :].bitcast(F32)
                 for g in range(2):
                     for u in range(2):
-                        c = 2 * g + u
-                        nc.tensor.transpose(out=bank[:, g, u, :], in_=words[:, c * P : (c + 1) * P], identity=ident_f32[:])
-                copies[l](out=vr_grouped[b, j][:].bitcast(F32)[:, l], in_=bank[:].rearrange("p g u k -> p g k u"))
-
-        def quantise_features(b, j):
+                        a = 2 * g + u
+                        nc.tensor.transpose(out=bank[:, g, u, :], in_=words[:, a * P : (a + 1) * P], identity=ident_f32[:])
+                copies[l](out=grouped[:].bitcast(F32)[:, l], in_=bank[:].rearrange("p g u k -> p g k u"))
             nc.vector.quantize_mx(
                 out=vr_codes[b][:, 2 * j : 2 * j + 2].rearrange("p l g k -> p (l g k)").bitcast(FP8X4),
                 scales=vr_scales[b][:, 2 * j : 2 * j + 2].rearrange("p l g k -> p (l g k)"),
-                in_=vr_grouped[b, j][:].rearrange("p l g k t -> p (l g k t)"),
+                in_=grouped[:].rearrange("p l g k t -> p (l g k t)"),
             )
 
         def project_values(b, n):
@@ -233,7 +231,7 @@ def tile_pgwcrossattention_pa_t_kernel(tc, q, k, v_ret, pi_star, Wv, bv, gamma, 
                 v_scales[b] = keep.tile([P, 2, H], U8, name="v_scales", align_bytes=64)
             if hc == 0:
                 v_grouped[b] = work.tile([P, H, PACK], BF16, name="v_grouped", tag="grouped", align_bytes=64)
-            bank = psum.tile([P, PACK, P], F32, name="v_bank", tag="mx")
+            bank = psum.tile([P, PACK, P], F32, name="v_bank", tag="mx" if n % 2 == 0 else "inputs")
             for t in range(PACK):
                 for g in range(2):
                     nc.tensor.matmul_mx(
@@ -259,7 +257,7 @@ def tile_pgwcrossattention_pa_t_kernel(tc, q, k, v_ret, pi_star, Wv, bv, gamma, 
 
         def logs(first, count):
             for i in range(first, first + count):
-                floor_stage(i, nc.gpsimd if i % 2 == 0 else nc.vector)
+                floor_stage(i)
                 log_stage(i)
 
         def first_scores(i):
@@ -267,12 +265,6 @@ def tile_pgwcrossattention_pa_t_kernel(tc, q, k, v_ret, pi_star, Wv, bv, gamma, 
             scores(i, 1)
             add_prior(i)
 
-        ones = const.tile([P, P], BF16)
-        nc.vector.memset(ones[:], 1.0)
-        rows = const.tile([P, H + GAMMA_COLS], BF16)
-        nc.vector.memset(rows[:], 0.0)
-        nc.scalar.dma_start(out=rows[0:1, 0:H], in_=bv.unsqueeze(0))
-        nc.scalar.dma_start(out=rows[0:1, H : H + 1], in_=gamma.unsqueeze(0))
         warm = const.tile([P, 1], F32)
         nc.vector.memset(warm[:], 1.0)
         nc.scalar.activation(out=warm[:], in_=warm[:], func=ACT.Ln)
@@ -281,59 +273,40 @@ def tile_pgwcrossattention_pa_t_kernel(tc, q, k, v_ret, pi_star, Wv, bv, gamma, 
         load_pi(1)
         load_k(0, 1)
         load_q(0)
+        load_q(1)
+        nc.sync.dma_start(out=gamma_bf[:], in_=gamma.partition_broadcast(P))
         load_pi(2)
         load_wv(0)
         load_pi(3)
         load_wv(1)
-        load_q(1)
-        bias_bank = psum.tile([P, H], F32, name="bias_bank", tag="inputs")
-        nc.tensor.matmul(out=bias_bank[:], lhsT=ones[:], rhs=rows[:, 0:H], start=True, stop=True)
-        nc.vector.tensor_copy(out=bias_bf[:], in_=bias_bank[:])
-        gamma_bank = psum.tile([P, GAMMA_COLS], F32, name="gamma_bank", tag="inputs")
-        nc.tensor.matmul(out=gamma_bank[:], lhsT=ones[:], rhs=rows[:, H : H + GAMMA_COLS], start=True, stop=True)
-        nc.vector.tensor_scalar(out=neg_gain[:], in0=gamma_bank[:, 0:1], scalar1=-math.sqrt(H), scalar2=None, op0=ALU.mult)
-        transpose_keys(0, 0, nc.scalar.copy)
-        transpose_keys(0, 1, nc.scalar.copy)
-        logs(0, 2)
+        logs(0, 4)
+        for j in range(4):
+            transpose_keys(0, j, nc.vector.tensor_copy)
+        nc.vector.tensor_scalar(out=neg_gain[:], in0=gamma_bf[:], scalar1=-math.sqrt(H), scalar2=None, op0=ALU.mult)
         load_pi(4)
         load_vr(0, 0)
-        transpose_keys(0, 2, nc.scalar.copy)
-        transpose_keys(0, 3, nc.scalar.copy)
-        logs(2, 2)
         load_pi(5)
         load_vr(0, 1)
-        logs(4, 2)
+        nc.sync.dma_start(out=bias_bf[:], in_=bv.partition_broadcast(P))
+        logs(4, 4)
         load_pi(6)
         load_vr(0, 2)
-        transpose_queries(0)
-        logs(6, 2)
         load_pi(7)
         load_vr(0, 3)
         load_q(2)
         load_q(3)
-        first_scores(0)
-        logs(8, 2)
-        first_scores(1)
+        transpose_queries(0)
         transpose_queries(1)
-        transpose_features(0, 0, (nc.scalar.copy, nc.scalar.copy))
-        logs(10, 2)
         quantise_weights(0)
-        transpose_features(0, 1, (nc.scalar.copy, nc.scalar.copy))
-        logs(12, 2)
-        quantise_features(0, 0)
-        first_scores(2)
-        transpose_features(0, 2, (nc.scalar.copy, nc.scalar.copy))
-        logs(14, 2)
-        for c in range(NB // 2, NB // 2 + 3):
-            load_pi(c)
-        for i in range(NB, NB + SPARE):
-            floor_stage(i, nc.gpsimd)
-        quantise_features(0, 1)
+        first_scores(0)
         quantise_weights(1)
-        first_scores(3)
-        transpose_features(0, 3, (nc.scalar.copy, nc.scalar.copy))
-        quantise_features(0, 2)
-        quantise_features(0, 3)
+        first_scores(1)
+        logs(8, 1)
+        for j in range(4):
+            transpose_features(0, j, (nc.scalar.copy, nc.scalar.copy))
+            if j < 2:
+                first_scores(2 + j)
+            logs(9 + 2 * j, min(2, NB - 9 - 2 * j))
         transpose_queries(AHEAD // 2)
         for n in range(8):
             project_values(0, n)
@@ -341,61 +314,58 @@ def tile_pgwcrossattention_pa_t_kernel(tc, q, k, v_ret, pi_star, Wv, bv, gamma, 
             exp_stage(i)
         transpose_probs(0)
 
-        def tile_of(t):
-            if t < 0 or NB - OWED <= t < NB:
+        def tile_of(tick):
+            if tick < 0 or NB - OWED <= tick < NB:
                 return -1
-            i = t if t < NB else t - OWED
+            i = tick if tick < NB else tick - OWED
             return i if i < TILES else -1
 
-        def beside_logs(i):
-            return NB - TURN <= i < NB - OWED
+        def regrouped_by_vector(i):
+            return NB - TURN <= i < NB - OWED or i >= TILES - LAST
 
-        def among_last(i):
-            return i >= TILES - LAST
-
-        for t in range(TILES + OWED + 1):
-            tt = t % NB
-            nb = t // NB + 1
-            turning = nb < B and tt >= NB - TURN
-            cur, prev, following = tile_of(t), tile_of(t - 1), tile_of(t + 1)
-            ahead = t + AHEAD
+        for tick in range(TILES + OWED + 1):
+            local = tick % NB
+            nb = tick // NB + 1
+            turning = nb < B and local >= NB - TURN
+            cur, prev, following = tile_of(tick), tile_of(tick - 1), tile_of(tick + 1)
+            ahead = tick + AHEAD
             if nb < B:
-                if tt < 2:
-                    load_k(nb, tt)
-                if 2 <= tt < 6:
-                    load_vr(nb, tt - 2)
-                if tt % 2 == 0 and tt < NB - SPARE - 2:
-                    load_pi((nb * NB + SPARE + tt + 2) // 2)
+                if local < 2:
+                    load_k(nb, local)
+                if local < 4:
+                    load_vr(nb, local)
+                if 1 <= local < 1 + NB // 2:
+                    load_pi(nb * NB // 2 + local - 1)
             if ahead % 2 == 0 and 2 * AHEAD <= ahead + AHEAD < TILES:
                 load_q((ahead + AHEAD) // 2)
-            if nb < B and tt < NB - SPARE:
-                floor_stage(nb * NB + SPARE + tt, nc.gpsimd)
+            if nb < B and FLOOR_TICK <= local < FLOOR_TICK + NB // 2:
+                floor_stage(nb * NB + 2 * (local - FLOOR_TICK))
+                floor_stage(nb * NB + 2 * (local - FLOOR_TICK) + 1)
             if cur >= 0:
-                regroup_probs(cur, nc.vector.tensor_copy if beside_logs(cur) or among_last(cur) else nc.scalar.copy)
-            if nb < B and KEYS_TICK <= tt < KEYS_TICK + 4:
-                transpose_keys(nb, tt - KEYS_TICK, nc.scalar.copy)
-            if (ahead + 1) % 2 == 0 and ahead + 1 < TILES:
-                transpose_queries((ahead + 1) // 2)
+                regroup_probs(cur, nc.vector.tensor_copy if regrouped_by_vector(cur) else nc.scalar.copy)
+            if nb < B and local % 2 == 0 and KEYS_TICK <= local < KEYS_TICK + 8:
+                transpose_keys(nb, (local - KEYS_TICK) // 2, nc.scalar.copy)
             if ahead < TILES:
                 scores(ahead, 0)
             if AHEAD <= ahead - 1 < TILES:
                 add_prior(ahead - 1)
             if cur >= 0:
                 quantise_probs(cur)
-            if nb < B and VALUES_TICK <= tt:
-                project_values(nb, 2 * (tt - VALUES_TICK))
-                project_values(nb, 2 * (tt - VALUES_TICK) + 1)
+            if nb < B and VALUES_TICK <= local:
+                project_values(nb, 2 * (local - VALUES_TICK))
+                project_values(nb, 2 * (local - VALUES_TICK) + 1)
             if prev >= 0:
                 weighted_values(prev)
             if ahead < TILES:
                 scores(ahead, 1)
-            if nb < B and FEATURES_TICK <= tt < FEATURES_TICK + 4:
-                transpose_features(nb, tt - FEATURES_TICK, (nc.scalar.copy, nc.vector.tensor_copy))
-                quantise_features(nb, tt - FEATURES_TICK)
+            if ahead % 2 == 0 and ahead + 2 < TILES:
+                transpose_queries((ahead + 2) // 2)
+            if nb < B and local % 2 == 1 and FEATURES_TICK <= local < FEATURES_TICK + 8:
+                transpose_features(nb, (local - FEATURES_TICK) // 2, (nc.scalar.copy, nc.vector.tensor_copy))
             if turning:
                 for n in range(NB // TURN):
-                    log_stage(nb * NB + (tt - (NB - TURN)) * (NB // TURN) + n)
-                if tt == NB - 1:
+                    log_stage(nb * NB + (local - (NB - TURN)) * (NB // TURN) + n)
+                if local == NB - 1:
                     for i in range(nb * NB - OWED, nb * NB):
                         exp_stage(i)
             elif cur >= 0 and cur + EXP_LEAD < TILES:
@@ -403,4 +373,4 @@ def tile_pgwcrossattention_pa_t_kernel(tc, q, k, v_ret, pi_star, Wv, bv, gamma, 
             if following >= 0:
                 transpose_probs(following)
             if prev >= 0:
-                normalise_and_store(prev, beside_logs(prev))
+                normalise_and_store(prev, turning)

@@ -42,7 +42,7 @@ def tile_pgwcrossattention_pa_t_kernel(tc, q, k, v_ret, pi_star, Wv, bv, gamma, 
     pi_view = pi_star.rearrange("b (n p) k -> p (b n) k", p=P)
     q_view = q.rearrange("b (n p) h -> p (b n) h", p=P)
     k_view = k.rearrange("b (n p) h -> p b n h", p=P)
-    vr_view = v_ret.rearrange("b (n p) d -> p b n d", p=P)
+    vr_view = v_ret.rearrange("b (a p y) d -> p b a y d", p=P, y=2)
     out_view = out.rearrange("b (n p) h -> p (b n) h", p=P)
     wv_view = Wv.rearrange("(a p y) h -> p a (y h)", a=4, y=2)
 
@@ -56,8 +56,6 @@ def tile_pgwcrossattention_pa_t_kernel(tc, q, k, v_ret, pi_star, Wv, bv, gamma, 
 
         ident_f32 = const.tile([P, P], F32)
         make_identity(nc, ident_f32[:])
-        ident_bf16 = const.tile([P, P], BF16)
-        make_identity(nc, ident_bf16[:])
         gamma_bf = const.tile([P, 1], BF16)
         bias_bf = const.tile([P, H], BF16)
         neg_gain = const.tile([P, 1], F32)
@@ -84,7 +82,7 @@ def tile_pgwcrossattention_pa_t_kernel(tc, q, k, v_ret, pi_star, Wv, bv, gamma, 
 
         def load_vr(b, j):
             vr_raw[b, j] = raw.tile([P, 2, DIN], BF16, name="vr_raw", tag="wide_raw", bufs=6)
-            nc.sync.dma_start(out=vr_raw[b, j][:], in_=vr_view[:, b, 2 * j : 2 * j + 2, :])
+            nc.sync.dma_start(out=vr_raw[b, j][:], in_=vr_view[:, b, j, :, :])
 
         def load_wv(g):
             wv_raw[g] = raw.tile([P, PACK, H], BF16, name="wv_raw", tag="wide_raw", bufs=6)
@@ -156,15 +154,16 @@ def tile_pgwcrossattention_pa_t_kernel(tc, q, k, v_ret, pi_star, Wv, bv, gamma, 
 
         def transpose_probs(i):
             if i >= TILES - LAST:
-                e_t[i] = psum.tile([P, KEY_TILES, P], BF16, name="e_t_last", tag="z", bufs=3)
+                e_t[i] = psum.tile([P, PACK, P], F32, name="e_t_last", tag="z", bufs=3)
             else:
-                e_t[i] = psum.tile([P, KEY_TILES, P], BF16, name="e_t", bufs=1)
-            for kt in range(KEY_TILES):
-                nc.tensor.transpose(out=e_t[i][:, kt, :], in_=e[i][:, kt * P : (kt + 1) * P], identity=ident_bf16[:])
+                e_t[i] = psum.tile([P, PACK, P], F32, name="e_t", bufs=1)
+            words = e[i][:].bitcast(F32)
+            for a in range(PACK):
+                nc.tensor.transpose(out=e_t[i][:, a, :], in_=words[:, a * P : (a + 1) * P], identity=ident_f32[:])
 
         def regroup_probs(i, copy):
             e_grouped[i] = work.tile([P, 2, P, PACK], BF16, name="e_grouped", align_bytes=64)
-            copy(out=e_grouped[i][:], in_=e_t[i][:].rearrange("p (c t) r -> p c r t", t=PACK))
+            copy(out=e_grouped[i][:].bitcast(F32), in_=e_t[i][:].rearrange("p (c u) r -> p c r u", u=2))
 
         def quantise_probs(i):
             e_codes[i] = work.tile([P, 2 * P], U32, name="e_codes", align_bytes=64)

@@ -65,7 +65,7 @@ def tile_pgwcrossattention_pa_t_kernel(tc, q, k, v_ret, pi_star, Wv, bv, gamma, 
         pi_raw, q_raw, k_raw, vr_raw, wv_raw = {}, {}, {}, {}, {}
         w, q_t, k_t, z = {}, {}, {}, {}
         e, e_t, e_grouped, e_codes, e_scales, acc = {}, {}, {}, {}, {}, {}
-        exp_bias, row_sum, row_recip = {}, {}, {}
+        w_min, exp_bias, row_sum, row_recip = {}, {}, {}, {}
         vr_codes, vr_scales, v_grouped, v_codes, v_scales = {}, {}, {}, {}, {}
 
         def load_pi(j):
@@ -139,10 +139,14 @@ def tile_pgwcrossattention_pa_t_kernel(tc, q, k, v_ret, pi_star, Wv, bv, gamma, 
                     out=w[i][:, cols], in0=w[i][:, cols], scalar=neg_gain[:, 0:1], in1=z[i, half][:],
                     op0=ALU.mult, op1=ALU.subtract,
                 )
-            w_min = work.tile([P, 1], F32, name="w_min")
-            nc.vector.tensor_reduce(out=w_min[:], in_=w[i][:], axis=AX.X, op=ALU.min)
+
+        def row_minimum(i):
+            w_min[i] = work.tile([P, 1], F32, name="w_min", bufs=8)
+            nc.vector.tensor_reduce(out=w_min[i][:], in_=w[i][:], axis=AX.X, op=ALU.min)
+
+        def scale_minimum(i):
             exp_bias[i] = work.tile([P, 1], F32, name="exp_bias", bufs=8)
-            nc.vector.tensor_scalar(out=exp_bias[i][:], in0=w_min[:], scalar1=inv_sqrt_h, scalar2=None, op0=ALU.mult)
+            nc.scalar.activation(out=exp_bias[i][:], in_=w_min[i][:], func=ACT.Copy, scale=inv_sqrt_h)
 
         def exp_stage(i):
             e[i] = work.tile([P, LK], BF16, name="e", bufs=EXP_LEAD + 3)
@@ -172,6 +176,8 @@ def tile_pgwcrossattention_pa_t_kernel(tc, q, k, v_ret, pi_star, Wv, bv, gamma, 
                 out=e_codes[i][:].bitcast(FP8X4), scales=e_scales[i][:],
                 in_=e_grouped[i][:].rearrange("p c r t -> p (c r t)"),
             )
+
+        def invert_sum(i):
             row_recip[i] = work.tile([P, 1], F32, name="row_recip", bufs=4)
             nc.vector.reciprocal(out=row_recip[i][:], in_=row_sum[i][:])
 
@@ -263,6 +269,7 @@ def tile_pgwcrossattention_pa_t_kernel(tc, q, k, v_ret, pi_star, Wv, bv, gamma, 
             scores(i, 0)
             scores(i, 1)
             add_prior(i)
+            row_minimum(i)
 
         warm = const.tile([P, 1], F32)
         nc.vector.memset(warm[:], 1.0)
@@ -310,6 +317,8 @@ def tile_pgwcrossattention_pa_t_kernel(tc, q, k, v_ret, pi_star, Wv, bv, gamma, 
         for n in range(8):
             project_values(0, n)
         for i in range(EXP_LEAD):
+            scale_minimum(i)
+        for i in range(EXP_LEAD):
             exp_stage(i)
         transpose_probs(0)
 
@@ -340,6 +349,11 @@ def tile_pgwcrossattention_pa_t_kernel(tc, q, k, v_ret, pi_star, Wv, bv, gamma, 
             if nb < B and FLOOR_TICK <= local < FLOOR_TICK + NB // 2:
                 floor_stage(nb * NB + 2 * (local - FLOOR_TICK))
                 floor_stage(nb * NB + 2 * (local - FLOOR_TICK) + 1)
+            if turning and local == NB - 1:
+                for i in range(nb * NB - OWED, nb * NB):
+                    scale_minimum(i)
+            elif not turning and cur >= 0 and cur + EXP_LEAD < TILES:
+                scale_minimum(cur + EXP_LEAD)
             if cur >= 0:
                 regroup_probs(cur, nc.vector.tensor_copy if regrouped_by_vector(cur) else nc.scalar.copy)
             if nb < B and local % 2 == 0 and KEYS_TICK <= local < KEYS_TICK + 8:
@@ -350,6 +364,10 @@ def tile_pgwcrossattention_pa_t_kernel(tc, q, k, v_ret, pi_star, Wv, bv, gamma, 
                 add_prior(ahead - 1)
             if cur >= 0:
                 quantise_probs(cur)
+            if AHEAD <= ahead - 1 < TILES:
+                row_minimum(ahead - 1)
+            if cur >= 0:
+                invert_sum(cur)
             if nb < B and VALUES_TICK <= local:
                 project_values(nb, 2 * (local - VALUES_TICK))
                 project_values(nb, 2 * (local - VALUES_TICK) + 1)

@@ -34,6 +34,7 @@ KEYS_TICK = 2
 FEATURES_TICK = 3
 VALUES_TICK = NB - TURN
 FLOOR_TICK = 4
+FLOOR_PIECES = 4
 
 
 def tile_pgwcrossattention_pa_t_kernel(tc, q, k, v_ret, pi_star, Wv, bv, gamma, out):
@@ -90,11 +91,14 @@ def tile_pgwcrossattention_pa_t_kernel(tc, q, k, v_ret, pi_star, Wv, bv, gamma, 
                 out=wv_raw[g][:].rearrange("p (u y) h -> p u (y h)", u=2), in_=wv_view[:, 2 * g : 2 * g + 2, :]
             )
 
-        def floor_stage(i):
+        def floor_stage(i, pieces=1):
             w[i] = keep.tile([P, LK], F32, name="w", bufs=NB + 4)
-            nc.gpsimd.tensor_scalar(
-                out=w[i][:], in0=pi_raw[i // 2][:, i % 2, :], scalar1=FLT_MAX, scalar2=FLOOR, op0=ALU.min, op1=ALU.max
-            )
+            for n in range(pieces):
+                cols = slice(n * LK // pieces, (n + 1) * LK // pieces)
+                nc.gpsimd.tensor_scalar(
+                    out=w[i][:, cols], in0=pi_raw[i // 2][:, i % 2, cols], scalar1=FLT_MAX, scalar2=FLOOR,
+                    op0=ALU.min, op1=ALU.max,
+                )
 
         def log_stage(i):
             nc.scalar.activation(out=w[i][:], in_=w[i][:], func=ACT.Ln)
@@ -347,8 +351,8 @@ def tile_pgwcrossattention_pa_t_kernel(tc, q, k, v_ret, pi_star, Wv, bv, gamma, 
             if ahead % 2 == 0 and 2 * AHEAD <= ahead + AHEAD < TILES:
                 load_q((ahead + AHEAD) // 2)
             if nb < B and FLOOR_TICK <= local < FLOOR_TICK + NB // 2:
-                floor_stage(nb * NB + 2 * (local - FLOOR_TICK))
-                floor_stage(nb * NB + 2 * (local - FLOOR_TICK) + 1)
+                floor_stage(nb * NB + 2 * (local - FLOOR_TICK), FLOOR_PIECES)
+                floor_stage(nb * NB + 2 * (local - FLOOR_TICK) + 1, FLOOR_PIECES)
             if turning and local == NB - 1:
                 for i in range(nb * NB - OWED, nb * NB):
                     scale_minimum(i)

@@ -105,13 +105,16 @@ def tile_pgwcrossattention_pa_t_kernel(tc, q, k, v_ret, pi_star, Wv, bv, gamma, 
 
         def transpose_keys(b, j, copy):
             if j == 0:
-                k_t[b] = keep.tile([P, 2, LK], F32, name="k_t")
+                k_t[b] = keep.tile([P, 2, 2, LK], BF16, name="k_t")
             bank = psum.tile([P, 2, 2, P], F32, name="k_bank", tag="inputs")
             for u in range(2):
                 for l in range(2):
                     words = k_raw[b, j // 2][:, 2 * (j % 2) + l, :].bitcast(F32)
                     nc.tensor.transpose(out=bank[:, u, l, :], in_=words[:, u * P : (u + 1) * P], identity=ident_f32[:])
-            copy(out=k_t[b][:, :, 2 * j * P : (2 * j + 2) * P], in_=bank[:].rearrange("p u l k -> p u (l k)"))
+            copy(
+                out=k_t[b][:, :, :, 2 * j * P : (2 * j + 2) * P],
+                in_=bank[:].rearrange("p u l k -> p u (l k)").bitcast(BF16).rearrange("p u (k y) -> p u y k", y=2),
+            )
 
         def transpose_queries(j):
             bank = psum.tile([P, 2, 2, P], F32, name="q_bank", tag="inputs")
@@ -123,7 +126,6 @@ def tile_pgwcrossattention_pa_t_kernel(tc, q, k, v_ret, pi_star, Wv, bv, gamma, 
             nc.vector.tensor_copy(out=q_t[j][:], in_=bank[:])
 
         def scores(i, half):
-            keys = k_t[i // NB][:].bitcast(BF16).rearrange("p u (k y) -> p u k y", y=2)
             z[i, half] = psum.tile([P, BANK], F32, name="z", bufs=3)
             for u in range(2):
                 rows = q_t[i // 2][:, i % 2, u, :].bitcast(BF16).rearrange("p (r y) -> p r y", y=2)
@@ -131,7 +133,7 @@ def tile_pgwcrossattention_pa_t_kernel(tc, q, k, v_ret, pi_star, Wv, bv, gamma, 
                     nc.tensor.matmul(
                         out=z[i, half][:],
                         lhsT=rows[:, :, y],
-                        rhs=keys[:, u, BANK * half : BANK * (half + 1), y],
+                        rhs=k_t[i // NB][:, u, y, BANK * half : BANK * (half + 1)],
                         start=(u == 0 and y == 0),
                         stop=(u == 1 and y == 1),
                     )

@@ -155,7 +155,7 @@ def tile_pgwcrossattention_pa_t_kernel(tc, q, k, v_ret, pi_star, Wv, bv, gamma, 
             nc.scalar.activation(out=exp_bias[i][:], in_=w_min[i][:], func=ACT.Copy, scale=inv_sqrt_h)
 
         def exp_stage(i):
-            e[i] = work.tile([P, LK], BF16, name="e", bufs=EXP_LEAD + 3)
+            e[i] = work.tile([P, LK], BF16, name="e", bufs=EXP_LEAD + OWED + 3)
             row_sum[i] = work.tile([P, 1], F32, name="row_sum", bufs=8)
             nc.scalar.activation(
                 out=e[i][:], in_=w[i][:], func=ACT.Exp, bias=exp_bias[i][:, 0:1], scale=-inv_sqrt_h,
@@ -337,6 +337,17 @@ def tile_pgwcrossattention_pa_t_kernel(tc, q, k, v_ret, pi_star, Wv, bv, gamma, 
         def regrouped_by_vector(i):
             return NB - TURN <= i < NB - OWED or i >= TILES - LAST
 
+        def exps_of(tick):
+            if tick < NB - TURN:
+                return [tick + EXP_LEAD]
+            if tick < NB - 1:
+                return []
+            if tick == NB - 1:
+                return list(range(NB - OWED, NB))
+            if tick < NB + OWED:
+                return [2 * tick - NB, 2 * tick - NB + 1]
+            return [tick + OWED] if tick + OWED < TILES else []
+
         for tick in range(TILES + OWED + 1):
             local = tick % NB
             nb = tick // NB + 1
@@ -355,11 +366,8 @@ def tile_pgwcrossattention_pa_t_kernel(tc, q, k, v_ret, pi_star, Wv, bv, gamma, 
             if nb < B and FLOOR_TICK <= local < FLOOR_TICK + NB // 2:
                 floor_stage(nb * NB + 2 * (local - FLOOR_TICK), FLOOR_PIECES)
                 floor_stage(nb * NB + 2 * (local - FLOOR_TICK) + 1, FLOOR_PIECES)
-            if turning and local == NB - 1:
-                for i in range(nb * NB - OWED, nb * NB):
-                    scale_minimum(i)
-            elif not turning and cur >= 0 and cur + EXP_LEAD < TILES:
-                scale_minimum(cur + EXP_LEAD)
+            for i in exps_of(tick):
+                scale_minimum(i)
             if cur >= 0:
                 regroup_probs(cur, nc.vector.tensor_copy if regrouped_by_vector(cur) else nc.scalar.copy)
             if nb < B and local % 2 == 0 and KEYS_TICK <= local < KEYS_TICK + 8:
@@ -388,11 +396,8 @@ def tile_pgwcrossattention_pa_t_kernel(tc, q, k, v_ret, pi_star, Wv, bv, gamma, 
             if turning:
                 for n in range(NB // TURN):
                     log_stage(nb * NB + (local - (NB - TURN)) * (NB // TURN) + n)
-                if local == NB - 1:
-                    for i in range(nb * NB - OWED, nb * NB):
-                        exp_stage(i)
-            elif cur >= 0 and cur + EXP_LEAD < TILES:
-                exp_stage(cur + EXP_LEAD)
+            for i in exps_of(tick):
+                exp_stage(i)
             if following >= 0:
                 transpose_probs(following)
             if prev >= 0:

@@ -35,6 +35,7 @@ FEATURES_TICK = 3
 VALUES_TICK = NB - TURN
 FLOOR_TICK = 4
 FLOOR_PIECES = 4
+LAST_PRIOR_TICK = TILES - AHEAD - 1
 
 
 def tile_pgwcrossattention_pa_t_kernel(tc, q, k, v_ret, pi_star, Wv, bv, gamma, out):
@@ -156,10 +157,11 @@ def tile_pgwcrossattention_pa_t_kernel(tc, q, k, v_ret, pi_star, Wv, bv, gamma, 
 
         def exp_stage(i):
             e[i] = work.tile([P, LK], BF16, name="e", bufs=EXP_LEAD + OWED + 3)
-            row_sum[i] = work.tile([P, 1], F32, name="row_sum", bufs=8)
+            if i % 2 == 0:
+                row_sum[i // 2] = work.tile([P, 2], F32, name="row_sum", bufs=4)
             nc.scalar.activation(
                 out=e[i][:], in_=w[i][:], func=ACT.Exp, bias=exp_bias[i][:, 0:1], scale=-inv_sqrt_h,
-                accum_out=row_sum[i][:, 0:1],
+                accum_out=row_sum[i // 2][:, i % 2 : i % 2 + 1],
             )
 
         def transpose_probs(i):
@@ -184,8 +186,9 @@ def tile_pgwcrossattention_pa_t_kernel(tc, q, k, v_ret, pi_star, Wv, bv, gamma, 
             )
 
         def invert_sum(i):
-            row_recip[i] = work.tile([P, 1], F32, name="row_recip", bufs=4)
-            nc.vector.reciprocal(out=row_recip[i][:], in_=row_sum[i][:])
+            if i % 2 == 0:
+                row_recip[i // 2] = work.tile([P, 2], F32, name="row_recip", bufs=3)
+                nc.vector.reciprocal(out=row_recip[i // 2][:], in_=row_sum[i // 2][:])
 
         def weighted_values(i):
             acc[i] = psum.tile([P, H], F32, name="acc", tag="mx")
@@ -201,11 +204,11 @@ def tile_pgwcrossattention_pa_t_kernel(tc, q, k, v_ret, pi_star, Wv, bv, gamma, 
                 )
 
         def normalise_and_store(i, on_vector):
-            o = work.tile([P, H], F32, name="o", bufs=4)
+            o = work.tile([P, H], F32, name="o", bufs=6)
             if on_vector:
-                nc.vector.tensor_scalar(out=o[:], in0=acc[i][:], scalar1=row_recip[i][:, 0:1], scalar2=None, op0=ALU.mult)
+                nc.vector.tensor_scalar(out=o[:], in0=acc[i][:], scalar1=row_recip[i // 2][:, i % 2 : i % 2 + 1], scalar2=None, op0=ALU.mult)
             else:
-                nc.scalar.activation(out=o[:], in_=acc[i][:], func=ACT.Copy, scale=row_recip[i][:, 0:1])
+                nc.scalar.activation(out=o[:], in_=acc[i][:], func=ACT.Copy, scale=row_recip[i // 2][:, i % 2 : i % 2 + 1])
             nc.sync.dma_start(out=out_view[:, i, :], in_=o[:])
 
         def quantise_weights(g):
@@ -348,12 +351,15 @@ def tile_pgwcrossattention_pa_t_kernel(tc, q, k, v_ret, pi_star, Wv, bv, gamma, 
                 return [2 * tick - NB, 2 * tick - NB + 1]
             return [tick + OWED] if tick + OWED < TILES else []
 
-        for tick in range(TILES + OWED + 1):
+        def ahead_of(tick):
+            return tick + AHEAD + (1 if tick >= NB - 1 else 0)
+
+        for tick in range(LAST_PRIOR_TICK + 1):
             local = tick % NB
             nb = tick // NB + 1
             turning = nb < B and local >= NB - TURN
             cur, prev, following = tile_of(tick), tile_of(tick - 1), tile_of(tick + 1)
-            ahead = tick + AHEAD
+            before, ahead = ahead_of(tick - 1), ahead_of(tick)
             if nb < B:
                 if local < 2:
                     load_k(nb, local)
@@ -361,25 +367,25 @@ def tile_pgwcrossattention_pa_t_kernel(tc, q, k, v_ret, pi_star, Wv, bv, gamma, 
                     load_vr(nb, local)
                 if 1 <= local < 1 + NB // 2:
                     load_pi(nb * NB // 2 + local - 1)
-            if ahead % 2 == 0 and 2 * AHEAD <= ahead + AHEAD < TILES:
-                load_q((ahead + AHEAD) // 2)
+            for j in range((before + AHEAD) // 2 + 1, min((ahead + AHEAD) // 2 + 1, TILES // 2)):
+                load_q(j)
             if nb < B and FLOOR_TICK <= local < FLOOR_TICK + NB // 2:
                 floor_stage(nb * NB + 2 * (local - FLOOR_TICK), FLOOR_PIECES)
                 floor_stage(nb * NB + 2 * (local - FLOOR_TICK) + 1, FLOOR_PIECES)
-            for i in exps_of(tick):
-                scale_minimum(i)
             if cur >= 0:
                 regroup_probs(cur, nc.vector.tensor_copy if regrouped_by_vector(cur) else nc.scalar.copy)
+            for i in exps_of(tick):
+                scale_minimum(i)
             if nb < B and local % 2 == 0 and KEYS_TICK <= local < KEYS_TICK + 8:
                 transpose_keys(nb, (local - KEYS_TICK) // 2, nc.scalar.copy)
-            if ahead < TILES:
-                scores(ahead, 0)
-            if AHEAD <= ahead - 1 < TILES:
-                add_prior(ahead - 1)
+            if before + 1 < TILES:
+                scores(before + 1, 0)
+            if AHEAD <= before < TILES:
+                add_prior(before)
             if cur >= 0:
                 quantise_probs(cur)
-            if AHEAD <= ahead - 1 < TILES:
-                row_minimum(ahead - 1)
+            if AHEAD <= before < TILES:
+                row_minimum(before)
             if cur >= 0:
                 invert_sum(cur)
             if nb < B and VALUES_TICK <= local:
@@ -387,18 +393,45 @@ def tile_pgwcrossattention_pa_t_kernel(tc, q, k, v_ret, pi_star, Wv, bv, gamma, 
                 project_values(nb, 2 * (local - VALUES_TICK) + 1)
             if prev >= 0:
                 weighted_values(prev)
-            if ahead < TILES:
+            if before + 1 < TILES:
+                scores(before + 1, 1)
+            if before + 1 < ahead < TILES:
+                scores(ahead, 0)
+                add_prior(before + 1)
+                row_minimum(before + 1)
                 scores(ahead, 1)
-            if ahead % 2 == 0 and ahead + 2 < TILES:
-                transpose_queries((ahead + 2) // 2)
-            if nb < B and local % 2 == 1 and FEATURES_TICK <= local < FEATURES_TICK + 8:
-                transpose_features(nb, (local - FEATURES_TICK) // 2, (nc.scalar.copy, nc.vector.tensor_copy))
             if turning:
                 for n in range(NB // TURN):
                     log_stage(nb * NB + (local - (NB - TURN)) * (NB // TURN) + n)
             for i in exps_of(tick):
                 exp_stage(i)
-            if following >= 0:
-                transpose_probs(following)
             if prev >= 0:
                 normalise_and_store(prev, turning)
+            for j in range((before + 2) // 2 + 1, min((ahead + 2) // 2 + 1, TILES // 2)):
+                transpose_queries(j)
+            if nb < B and local % 2 == 1 and FEATURES_TICK <= local < FEATURES_TICK + 8:
+                transpose_features(nb, (local - FEATURES_TICK) // 2, (nc.scalar.copy, nc.vector.tensor_copy))
+            if following >= 0:
+                transpose_probs(following)
+
+        first = tile_of(LAST_PRIOR_TICK) + 1
+        for tick in range(LAST_PRIOR_TICK + 1, TILES + OWED + 1):
+            for i in exps_of(tick):
+                scale_minimum(i)
+                exp_stage(i)
+        regroup_probs(first, nc.vector.tensor_copy)
+        invert_sum(first)
+        weighted_values(first - 1)
+        transpose_probs(first + 1)
+        normalise_and_store(first - 1, False)
+        for i in range(first + 1, TILES):
+            regroup_probs(i, nc.vector.tensor_copy)
+            quantise_probs(i - 1)
+            invert_sum(i)
+            if i + 1 < TILES:
+                transpose_probs(i + 1)
+            weighted_values(i - 1)
+            normalise_and_store(i - 1, False)
+        quantise_probs(TILES - 1)
+        weighted_values(TILES - 1)
+        normalise_and_store(TILES - 1, False)

@@ -25,17 +25,21 @@ TILES = B * NB
 KEY_TILES = LK // P
 BANK = 512
 
-AHEAD = 4
-EXP_LEAD = 2
-TURN = 4
-OWED = 2
-LAST = 4
-KEYS_TICK = 2
-FEATURES_TICK = 3
-VALUES_TICK = NB - TURN
-FLOOR_TICK = 4
-FLOOR_PIECES = 4
-LAST_PRIOR_TICK = TILES - AHEAD - 1
+
+LEAD = 14
+LOG_TICKS = 13
+WEIGHT_TICK = (3, 6)
+WLOAD = (1, 4)
+FEATURES_TICK = (2, 15)
+FEATURES_STEP = (1, 1)
+VALUES_TICK = (7, 20)
+KEYS_TICK = 8
+KEYS_STEP = 2
+KEYS_VECTOR = 0
+FEATURES_VECTOR = (0, 1)
+MX_LAG = 2
+TAIL_MOD = 2
+LAST_PRIOR_TICK = TILES - LEAD
 
 
 def tile_pgwcrossattention_pa_t_kernel(tc, q, k, v_ret, pi_star, Wv, bv, gamma, out):
@@ -50,11 +54,11 @@ def tile_pgwcrossattention_pa_t_kernel(tc, q, k, v_ret, pi_star, Wv, bv, gamma, 
 
     with ExitStack() as ctx:
         const = ctx.enter_context(tc.tile_pool(name="const", bufs=1))
-        raw = ctx.enter_context(tc.tile_pool(name="raw", bufs=4))
+        raw = ctx.enter_context(tc.tile_pool(name="raw", bufs=2))
         keep = ctx.enter_context(tc.tile_pool(name="keep", bufs=2))
-        work = ctx.enter_context(tc.tile_pool(name="work", bufs=3))
+        work = ctx.enter_context(tc.tile_pool(name="work", bufs=2))
         psum = ctx.enter_context(tc.psum_pool(name="psum", bufs=2))
-        ctx.enter_context(tc.manual_schedule())
+        ctx.enter_context(tc.manual_schedule(engines={mybir.EngineType.Activation}))
 
         ident_f32 = const.tile([P, P], F32)
         make_identity(nc, ident_f32[:])
@@ -65,17 +69,18 @@ def tile_pgwcrossattention_pa_t_kernel(tc, q, k, v_ret, pi_star, Wv, bv, gamma, 
         wv_scales = const.tile([P, 2, H], U8, align_bytes=64)
 
         pi_raw, q_raw, k_raw, vr_raw, wv_raw = {}, {}, {}, {}, {}
+        k_bank, q_bank, vr_bank, v_bank = {}, {}, {}, {}
         w, q_t, k_t, z = {}, {}, {}, {}
         e, e_t, e_grouped, e_codes, e_scales, acc = {}, {}, {}, {}, {}, {}
         w_min, exp_bias, row_sum, row_recip = {}, {}, {}, {}
-        vr_codes, vr_scales, v_grouped, v_codes, v_scales = {}, {}, {}, {}, {}
+        wv_grouped, vr_grouped, vr_codes, vr_scales, v_grouped, v_codes, v_scales = {}, {}, {}, {}, {}, {}, {}
 
         def load_pi(j):
-            pi_raw[j] = raw.tile([P, 2, LK], BF16, name="pi_raw")
+            pi_raw[j] = raw.tile([P, 2, LK], BF16, name="pi_raw", bufs=3)
             nc.sync.dma_start(out=pi_raw[j][:], in_=pi_view[:, 2 * j : 2 * j + 2, :])
 
         def load_q(j):
-            q_raw[j] = raw.tile([P, 2, H], BF16, name="q_raw")
+            q_raw[j] = raw.tile([P, 2, H], BF16, name="q_raw", bufs=2)
             nc.sync.dma_start(out=q_raw[j][:], in_=q_view[:, 2 * j : 2 * j + 2, :])
 
         def load_k(b, half):
@@ -83,38 +88,38 @@ def tile_pgwcrossattention_pa_t_kernel(tc, q, k, v_ret, pi_star, Wv, bv, gamma, 
             nc.sync.dma_start(out=k_raw[b, half][:], in_=k_view[:, b, 4 * half : 4 * half + 4, :])
 
         def load_vr(b, j):
-            vr_raw[b, j] = raw.tile([P, 2, DIN], BF16, name="vr_raw", tag="wide_raw", bufs=6)
+            vr_raw[b, j] = raw.tile([P, 2, DIN], BF16, name="vr_raw", tag="wide_raw", bufs=3)
             nc.sync.dma_start(out=vr_raw[b, j][:], in_=vr_view[:, b, j, :, :])
 
         def load_wv(g):
-            wv_raw[g] = raw.tile([P, PACK, H], BF16, name="wv_raw", tag="wide_raw", bufs=6)
+            wv_raw[g] = raw.tile([P, PACK, H], BF16, name="wv_raw", tag="wide_raw", bufs=3)
             nc.sync.dma_start(
                 out=wv_raw[g][:].rearrange("p (u y) h -> p u (y h)", u=2), in_=wv_view[:, 2 * g : 2 * g + 2, :]
             )
 
-        def floor_stage(i, pieces=1):
-            w[i] = keep.tile([P, LK], F32, name="w", bufs=NB + 4)
-            for n in range(pieces):
-                cols = slice(n * LK // pieces, (n + 1) * LK // pieces)
-                nc.gpsimd.tensor_scalar(
-                    out=w[i][:, cols], in0=pi_raw[i // 2][:, i % 2, cols], scalar1=FLT_MAX, scalar2=FLOOR,
-                    op0=ALU.min, op1=ALU.max,
-                )
+        def floor_stage(i):
+            w[i] = keep.tile([P, LK], F32, name="w", tag="w", bufs=TILES + 1)
+            nc.gpsimd.tensor_scalar(
+                out=w[i][:], in0=pi_raw[i // 2][:, i % 2, :], scalar1=FLT_MAX, scalar2=FLOOR, op0=ALU.min, op1=ALU.max
+            )
 
         def log_stage(i):
             nc.scalar.activation(out=w[i][:], in_=w[i][:], func=ACT.Ln)
 
-        def transpose_keys(b, j, copy):
-            if j == 0:
-                k_t[b] = keep.tile([P, 2, 2, LK], BF16, name="k_t")
+        def transpose_keys(b, j):
             bank = psum.tile([P, 2, 2, P], F32, name="k_bank", tag="inputs")
             for u in range(2):
                 for l in range(2):
                     words = k_raw[b, j // 2][:, 2 * (j % 2) + l, :].bitcast(F32)
                     nc.tensor.transpose(out=bank[:, u, l, :], in_=words[:, u * P : (u + 1) * P], identity=ident_f32[:])
+            k_bank[b, j] = bank
+
+        def copy_keys(b, j, copy):
+            if j == 0:
+                k_t[b] = keep.tile([P, 2, 2, LK], BF16, name="k_t")
             copy(
                 out=k_t[b][:, :, :, 2 * j * P : (2 * j + 2) * P],
-                in_=bank[:].rearrange("p u l k -> p u (l k)").bitcast(BF16).rearrange("p u (k y) -> p u y k", y=2),
+                in_=k_bank[b, j][:].rearrange("p u l k -> p u (l k)").bitcast(BF16).rearrange("p u (k y) -> p u y k", y=2),
             )
 
         def transpose_queries(j):
@@ -123,8 +128,11 @@ def tile_pgwcrossattention_pa_t_kernel(tc, q, k, v_ret, pi_star, Wv, bv, gamma, 
                 words = q_raw[j][:, l, :].bitcast(F32)
                 for u in range(2):
                     nc.tensor.transpose(out=bank[:, l, u, :], in_=words[:, u * P : (u + 1) * P], identity=ident_f32[:])
+            q_bank[j] = bank
+
+        def copy_queries(j, copy):
             q_t[j] = work.tile([P, 2, 2, P], F32, name="q_t")
-            nc.vector.tensor_copy(out=q_t[j][:], in_=bank[:])
+            copy(out=q_t[j][:], in_=q_bank[j][:])
 
         def scores(i, half):
             z[i, half] = psum.tile([P, BANK], F32, name="z", bufs=3)
@@ -148,24 +156,24 @@ def tile_pgwcrossattention_pa_t_kernel(tc, q, k, v_ret, pi_star, Wv, bv, gamma, 
                 )
 
         def row_minimum(i):
-            w_min[i] = work.tile([P, 1], F32, name="w_min", bufs=8)
+            w_min[i] = work.tile([P, 1], F32, name="w_min", bufs=LEAD + 3)
             nc.vector.tensor_reduce(out=w_min[i][:], in_=w[i][:], axis=AX.X, op=ALU.min)
 
         def scale_minimum(i):
-            exp_bias[i] = work.tile([P, 1], F32, name="exp_bias", bufs=8)
+            exp_bias[i] = work.tile([P, 1], F32, name="exp_bias", bufs=4)
             nc.scalar.activation(out=exp_bias[i][:], in_=w_min[i][:], func=ACT.Copy, scale=inv_sqrt_h)
 
         def exp_stage(i):
-            e[i] = work.tile([P, LK], BF16, name="e", bufs=EXP_LEAD + OWED + 3)
+            e[i] = keep.tile([P, LK], BF16, name="e", tag="w", bufs=TILES + 1)
             if i % 2 == 0:
-                row_sum[i // 2] = work.tile([P, 2], F32, name="row_sum", bufs=4)
+                row_sum[i // 2] = work.tile([P, 2], F32, name="row_sum", bufs=8)
             nc.scalar.activation(
                 out=e[i][:], in_=w[i][:], func=ACT.Exp, bias=exp_bias[i][:, 0:1], scale=-inv_sqrt_h,
                 accum_out=row_sum[i // 2][:, i % 2 : i % 2 + 1],
             )
 
         def transpose_probs(i):
-            if i >= TILES - LAST:
+            if i > LAST_PRIOR_TICK + 1:
                 e_t[i] = psum.tile([P, PACK, P], F32, name="e_t_last", tag="z", bufs=3)
             else:
                 e_t[i] = psum.tile([P, PACK, P], F32, name="e_t", bufs=1)
@@ -178,8 +186,8 @@ def tile_pgwcrossattention_pa_t_kernel(tc, q, k, v_ret, pi_star, Wv, bv, gamma, 
             copy(out=e_grouped[i][:].bitcast(F32), in_=e_t[i][:].rearrange("p (c u) r -> p c r u", u=2))
 
         def quantise_probs(i):
-            e_codes[i] = work.tile([P, 2 * P], U32, name="e_codes", align_bytes=64)
-            e_scales[i] = work.tile([P, 2 * P], U8, name="e_scales", align_bytes=64)
+            e_codes[i] = work.tile([P, 2 * P], U32, name="e_codes", bufs=3, align_bytes=64)
+            e_scales[i] = work.tile([P, 2 * P], U8, name="e_scales", bufs=3, align_bytes=64)
             nc.vector.quantize_mx(
                 out=e_codes[i][:].bitcast(FP8X4), scales=e_scales[i][:],
                 in_=e_grouped[i][:].rearrange("p c r t -> p (c r t)"),
@@ -187,7 +195,7 @@ def tile_pgwcrossattention_pa_t_kernel(tc, q, k, v_ret, pi_star, Wv, bv, gamma, 
 
         def invert_sum(i):
             if i % 2 == 0:
-                row_recip[i // 2] = work.tile([P, 2], F32, name="row_recip", bufs=3)
+                row_recip[i // 2] = work.tile([P, 2], F32, name="row_recip", bufs=4)
                 nc.vector.reciprocal(out=row_recip[i // 2][:], in_=row_sum[i // 2][:])
 
         def weighted_values(i):
@@ -204,48 +212,52 @@ def tile_pgwcrossattention_pa_t_kernel(tc, q, k, v_ret, pi_star, Wv, bv, gamma, 
                 )
 
         def normalise_and_store(i, on_vector):
-            o = work.tile([P, H], F32, name="o", bufs=6)
+            o = work.tile([P, H], F32, name="o", bufs=4)
             if on_vector:
                 nc.vector.tensor_scalar(out=o[:], in0=acc[i][:], scalar1=row_recip[i // 2][:, i % 2 : i % 2 + 1], scalar2=None, op0=ALU.mult)
             else:
                 nc.scalar.activation(out=o[:], in_=acc[i][:], func=ACT.Copy, scale=row_recip[i // 2][:, i % 2 : i % 2 + 1])
             nc.sync.dma_start(out=out_view[:, i, :], in_=o[:])
 
+        def group_weights(g):
+            wv_grouped[g] = work.tile([P, H, PACK], BF16, name="wv_grouped", tag="grouped", align_bytes=64)
+            nc.vector.tensor_copy(out=wv_grouped[g][:], in_=wv_raw[g][:].rearrange("p t h -> p h t"))
+
         def quantise_weights(g):
-            grouped = work.tile([P, H, PACK], BF16, name="wv_grouped", tag="grouped", align_bytes=64)
-            nc.vector.tensor_copy(out=grouped[:], in_=wv_raw[g][:].rearrange("p t h -> p h t"))
             nc.vector.quantize_mx(
-                out=wv_codes[:, g, :].bitcast(FP8X4), scales=wv_scales[:, g, :], in_=grouped[:].rearrange("p h t -> p (h t)")
+                out=wv_codes[:, g, :].bitcast(FP8X4), scales=wv_scales[:, g, :], in_=wv_grouped[g][:].rearrange("p h t -> p (h t)")
             )
 
-        def transpose_features(b, j, copies):
+        def transpose_features(b, n, tag):
+            bank = psum.tile([P, 2, 2, P], F32, name="vr_bank", tag=tag)
+            words = vr_raw[b, n // 2][:, n % 2, :].bitcast(F32)
+            for g in range(2):
+                for u in range(2):
+                    a = 2 * g + u
+                    nc.tensor.transpose(out=bank[:, g, u, :], in_=words[:, a * P : (a + 1) * P], identity=ident_f32[:])
+            vr_bank[b, n] = bank
+
+        def copy_features(b, n, copy):
+            if n % 2 == 0:
+                vr_grouped[b, n // 2] = work.tile([P, 2, 2, P, PACK], BF16, name="vr_grouped", tag="grouped", align_bytes=64)
+            copy(
+                out=vr_grouped[b, n // 2][:].bitcast(F32)[:, n % 2], in_=vr_bank[b, n][:].rearrange("p g u k -> p g k u")
+            )
+
+        def quantise_features(b, j):
             if j == 0:
                 vr_codes[b] = keep.tile([P, KEY_TILES, 2, P], U32, name="vr_codes", bufs=1, align_bytes=64)
                 vr_scales[b] = keep.tile([P, KEY_TILES, 2, P], U8, name="vr_scales", bufs=1, align_bytes=64)
-            grouped = work.tile([P, 2, 2, P, PACK], BF16, name="vr_grouped", tag="grouped", align_bytes=64)
-            for l in range(2):
-                bank = psum.tile([P, 2, 2, P], F32, name="vr_bank", tag="inputs")
-                words = vr_raw[b, j][:, l, :].bitcast(F32)
-                for g in range(2):
-                    for u in range(2):
-                        a = 2 * g + u
-                        nc.tensor.transpose(out=bank[:, g, u, :], in_=words[:, a * P : (a + 1) * P], identity=ident_f32[:])
-                copies[l](out=grouped[:].bitcast(F32)[:, l], in_=bank[:].rearrange("p g u k -> p g k u"))
             nc.vector.quantize_mx(
                 out=vr_codes[b][:, 2 * j : 2 * j + 2].rearrange("p l g k -> p (l g k)").bitcast(FP8X4),
                 scales=vr_scales[b][:, 2 * j : 2 * j + 2].rearrange("p l g k -> p (l g k)"),
-                in_=grouped[:].rearrange("p l g k t -> p (l g k t)"),
+                in_=vr_grouped[b, j][:].rearrange("p l g k t -> p (l g k t)"),
             )
 
-        def project_values(b, n):
+        def project_values(b, n, tag):
             c, hc = n // 4, n % 4
             cols = slice(hc * P, (hc + 1) * P)
-            if n == 0:
-                v_codes[b] = keep.tile([P, 2, H], U32, name="v_codes", align_bytes=64)
-                v_scales[b] = keep.tile([P, 2, H], U8, name="v_scales", align_bytes=64)
-            if hc == 0:
-                v_grouped[b] = work.tile([P, H, PACK], BF16, name="v_grouped", tag="grouped", align_bytes=64)
-            bank = psum.tile([P, PACK, P], F32, name="v_bank", tag="mx" if n % 2 == 0 else "inputs")
+            bank = psum.tile([P, PACK, P], F32, name="v_bank", tag=tag)
             for t in range(PACK):
                 for g in range(2):
                     nc.tensor.matmul_mx(
@@ -257,181 +269,174 @@ def tile_pgwcrossattention_pa_t_kernel(tc, q, k, v_ret, pi_star, Wv, bv, gamma, 
                         start=(g == 0),
                         stop=(g == 1),
                     )
+            v_bank[b, n] = bank
+
+        def add_bias(b, n):
+            c, hc = n // 4, n % 4
+            cols = slice(hc * P, (hc + 1) * P)
+            if n == 0:
+                v_codes[b] = keep.tile([P, 2, H], U32, name="v_codes", align_bytes=64)
+                v_scales[b] = keep.tile([P, 2, H], U8, name="v_scales", align_bytes=64)
+            if hc == 0:
+                v_grouped[b, c] = work.tile([P, H, PACK], BF16, name="v_grouped", tag="grouped", align_bytes=64)
             nc.vector.tensor_tensor(
-                out=v_grouped[b][:, cols, :],
-                in0=bank[:].rearrange("p t h -> p h t"),
+                out=v_grouped[b, c][:, cols, :],
+                in0=v_bank[b, n][:].rearrange("p t h -> p h t"),
                 in1=bias_bf[:, cols].unsqueeze(2).to_broadcast([P, P, PACK]),
                 op=ALU.add,
             )
-            if hc == 3:
-                nc.vector.quantize_mx(
-                    out=v_codes[b][:, c, :].bitcast(FP8X4), scales=v_scales[b][:, c, :],
-                    in_=v_grouped[b][:].rearrange("p h t -> p (h t)"),
-                )
 
-        def logs(first, count):
-            for i in range(first, first + count):
-                floor_stage(i)
-                log_stage(i)
+        def quantise_values(b, c):
+            nc.vector.quantize_mx(
+                out=v_codes[b][:, c, :].bitcast(FP8X4), scales=v_scales[b][:, c, :],
+                in_=v_grouped[b, c][:].rearrange("p h t -> p (h t)"),
+            )
 
-        def first_scores(i):
-            scores(i, 0)
-            scores(i, 1)
-            add_prior(i)
-            row_minimum(i)
+        def logs_until(h):
+            return max(0, min(TILES, -(-TILES * (h + 1) // LOG_TICKS)))
+
+        def exps_until(h):
+            return max(0, min(TILES, h - 1, (3 * (h - LEAD + 2) + 1) // 2))
 
         warm = const.tile([P, 1], F32)
         nc.vector.memset(warm[:], 1.0)
         nc.scalar.activation(out=warm[:], in_=warm[:], func=ACT.Ln)
         load_pi(0)
         load_k(0, 0)
-        load_pi(1)
-        load_k(0, 1)
         load_q(0)
+        load_k(0, 1)
+        load_pi(1)
         load_q(1)
         nc.sync.dma_start(out=gamma_bf[:], in_=gamma.partition_broadcast(P))
         load_pi(2)
-        load_wv(0)
-        load_pi(3)
-        load_wv(1)
-        logs(0, 4)
-        for j in range(4):
-            transpose_keys(0, j, nc.vector.tensor_copy)
-        nc.vector.tensor_scalar(out=neg_gain[:], in0=gamma_bf[:], scalar1=-math.sqrt(H), scalar2=None, op0=ALU.mult)
-        load_pi(4)
-        load_vr(0, 0)
-        load_pi(5)
-        load_vr(0, 1)
-        nc.sync.dma_start(out=bias_bf[:], in_=bv.partition_broadcast(P))
-        logs(4, 4)
-        load_pi(6)
-        load_vr(0, 2)
-        load_pi(7)
-        load_vr(0, 3)
-        load_q(2)
-        load_q(3)
+        loaded = 3
+        floor_stage(0)
+        floor_stage(1)
+        log_stage(0)
+        transpose_keys(0, 0)
+        transpose_keys(0, 1)
+        copy_keys(0, 0, nc.vector.tensor_copy)
+        copy_keys(0, 1, nc.vector.tensor_copy)
         transpose_queries(0)
-        transpose_queries(1)
-        quantise_weights(0)
-        first_scores(0)
-        quantise_weights(1)
-        first_scores(1)
-        logs(8, 1)
-        for j in range(4):
-            transpose_features(0, j, (nc.scalar.copy, nc.scalar.copy))
-            if j < 2:
-                first_scores(2 + j)
-            logs(9 + 2 * j, min(2, NB - 9 - 2 * j))
-        transpose_queries(AHEAD // 2)
-        for n in range(8):
-            project_values(0, n)
-        for i in range(EXP_LEAD):
-            scale_minimum(i)
-        for i in range(EXP_LEAD):
-            exp_stage(i)
-        transpose_probs(0)
+        copy_queries(0, nc.vector.tensor_copy)
+        log_stage(1)
+        transpose_keys(0, 2)
+        transpose_keys(0, 3)
+        copy_keys(0, 2, nc.scalar.copy)
+        copy_keys(0, 3, nc.scalar.copy)
+        nc.vector.tensor_scalar(out=neg_gain[:], in0=gamma_bf[:], scalar1=-math.sqrt(H), scalar2=None, op0=ALU.mult)
 
-        def tile_of(tick):
-            if tick < 0 or NB - OWED <= tick < NB:
-                return -1
-            i = tick if tick < NB else tick - OWED
-            return i if i < TILES else -1
-
-        def regrouped_by_vector(i):
-            return NB - TURN <= i < NB - OWED or i >= TILES - LAST
-
-        def exps_of(tick):
-            if tick < NB - TURN:
-                return [tick + EXP_LEAD]
-            if tick < NB - 1:
-                return []
-            if tick == NB - 1:
-                return list(range(NB - OWED, NB))
-            if tick < NB + OWED:
-                return [2 * tick - NB, 2 * tick - NB + 1]
-            return [tick + OWED] if tick + OWED < TILES else []
-
-        def ahead_of(tick):
-            return tick + AHEAD + (1 if tick >= NB - 1 else 0)
-
-        for tick in range(LAST_PRIOR_TICK + 1):
-            local = tick % NB
-            nb = tick // NB + 1
-            turning = nb < B and local >= NB - TURN
-            cur, prev, following = tile_of(tick), tile_of(tick - 1), tile_of(tick + 1)
-            before, ahead = ahead_of(tick - 1), ahead_of(tick)
-            if nb < B:
-                if local < 2:
-                    load_k(nb, local)
-                if local < 4:
-                    load_vr(nb, local)
-                if 1 <= local < 1 + NB // 2:
-                    load_pi(nb * NB // 2 + local - 1)
-            for j in range((before + AHEAD) // 2 + 1, min((ahead + AHEAD) // 2 + 1, TILES // 2)):
-                load_q(j)
-            if nb < B and FLOOR_TICK <= local < FLOOR_TICK + NB // 2:
-                floor_stage(nb * NB + 2 * (local - FLOOR_TICK), FLOOR_PIECES)
-                floor_stage(nb * NB + 2 * (local - FLOOR_TICK) + 1, FLOOR_PIECES)
-            if cur >= 0:
-                regroup_probs(cur, nc.vector.tensor_copy if regrouped_by_vector(cur) else nc.scalar.copy)
-            for i in exps_of(tick):
+        for h in range(TILES + 1):
+            tick = h - LEAD
+            cur, mul, div, following, new = tick, tick - MX_LAG, tick - MX_LAG - 1, tick + 1, h
+            exps = list(range(exps_until(h - 1), exps_until(h)))
+            logs = list(range(max(2, logs_until(h - 1)), logs_until(h)))
+            for i in logs:
+                floor_stage(i)
+            while loaded < min(NB, logs_until(h) // 2 + 3):
+                load_pi(loaded)
+                loaded += 1
+            if h % 2 == 0 and 2 <= h // 2 + 2 < NB:
+                load_q(h // 2 + 2)
+            if h in WLOAD:
+                load_wv(WLOAD.index(h))
+            if h == WLOAD[1]:
+                nc.sync.dma_start(out=bias_bf[:], in_=bv.partition_broadcast(P))
+            for b in range(B):
+                n = h + 2 - FEATURES_TICK[b]
+                if n % 2 == 0 and 0 <= n // 2 < 4:
+                    load_vr(b, n // 2)
+            if h + 3 - KEYS_TICK in (0, 1):
+                load_k(1, h + 3 - KEYS_TICK)
+            if new < TILES:
+                scores(new, 0)
+            for i in logs[:1]:
+                log_stage(i)
+            for i in exps[:1]:
                 scale_minimum(i)
-            if nb < B and local % 2 == 0 and KEYS_TICK <= local < KEYS_TICK + 8:
-                transpose_keys(nb, (local - KEYS_TICK) // 2, nc.scalar.copy)
-            if before + 1 < TILES:
-                scores(before + 1, 0)
-            if AHEAD <= before < TILES:
-                add_prior(before)
+                exp_stage(i)
+            if cur >= 0:
+                regroup_probs(cur, nc.scalar.copy)
+            if div >= 0:
+                normalise_and_store(div, False)
+            if new >= 1:
+                add_prior(new - 1)
+            if h % 2 == 1 and (h + 1) // 2 < NB:
+                copy_queries((h + 1) // 2, nc.vector.tensor_copy)
+            if h - 1 in WEIGHT_TICK:
+                quantise_weights(WEIGHT_TICK.index(h - 1))
+            for b in range(B):
+                n = h - 2 - FEATURES_TICK[b]
+                if n % 2 == 1 and 0 <= n < 8:
+                    quantise_features(b, n // 2)
+            for b in range(B):
+                n = h - 2 - VALUES_TICK[b]
+                if n in (3, 7):
+                    quantise_values(b, n // 4)
+            if new >= 1:
+                row_minimum(new - 1)
+            n, r = divmod(h - 1 - KEYS_TICK, KEYS_STEP)
+            if r == 0 and 0 <= n < 4:
+                copy_keys(1, n, nc.vector.tensor_copy if n < KEYS_VECTOR else nc.scalar.copy)
+            for b in range(B):
+                n = h - 1 - FEATURES_TICK[b]
+                if 0 <= n < 8:
+                    copy_features(b, n, nc.vector.tensor_copy if n % 2 < FEATURES_VECTOR[b] else nc.scalar.copy)
+            for b in range(B):
+                n = h - 1 - VALUES_TICK[b]
+                if 0 <= n < 8:
+                    add_bias(b, n)
             if cur >= 0:
                 quantise_probs(cur)
-            if AHEAD <= before < TILES:
-                row_minimum(before)
-            if cur >= 0:
                 invert_sum(cur)
-            if nb < B and VALUES_TICK <= local:
-                project_values(nb, 2 * (local - VALUES_TICK))
-                project_values(nb, 2 * (local - VALUES_TICK) + 1)
-            if prev >= 0:
-                weighted_values(prev)
-            if before + 1 < TILES:
-                scores(before + 1, 1)
-            if before + 1 < ahead < TILES:
-                scores(ahead, 0)
-                add_prior(before + 1)
-                row_minimum(before + 1)
-                scores(ahead, 1)
-            if turning:
-                for n in range(NB // TURN):
-                    log_stage(nb * NB + (local - (NB - TURN)) * (NB // TURN) + n)
-            for i in exps_of(tick):
+            if h in WEIGHT_TICK:
+                group_weights(WEIGHT_TICK.index(h))
+            for i in logs[1:]:
+                log_stage(i)
+            for i in exps[1:]:
+                scale_minimum(i)
                 exp_stage(i)
-            if prev >= 0:
-                normalise_and_store(prev, turning)
-            for j in range((before + 2) // 2 + 1, min((ahead + 2) // 2 + 1, TILES // 2)):
-                transpose_queries(j)
-            if nb < B and local % 2 == 1 and FEATURES_TICK <= local < FEATURES_TICK + 8:
-                transpose_features(nb, (local - FEATURES_TICK) // 2, (nc.scalar.copy, nc.vector.tensor_copy))
+            if mul >= 0:
+                weighted_values(mul)
+            for b in range(B):
+                n = h - VALUES_TICK[b]
+                if 0 <= n < 8:
+                    project_values(b, n, "mx")
+            if new < TILES:
+                scores(new, 1)
+            for b in range(B):
+                n = h - FEATURES_TICK[b]
+                if 0 <= n < 8:
+                    transpose_features(b, n, "inputs" if b else "mx")
+            if h % 2 == 0 and h // 2 + 1 < NB:
+                transpose_queries(h // 2 + 1)
+            n, r = divmod(h - KEYS_TICK, KEYS_STEP)
+            if r == 0 and 0 <= n < 4:
+                transpose_keys(1, n)
             if following >= 0:
                 transpose_probs(following)
 
-        first = tile_of(LAST_PRIOR_TICK) + 1
-        for tick in range(LAST_PRIOR_TICK + 1, TILES + OWED + 1):
-            for i in exps_of(tick):
-                scale_minimum(i)
-                exp_stage(i)
-        regroup_probs(first, nc.vector.tensor_copy)
-        invert_sum(first)
-        weighted_values(first - 1)
+        first = LAST_PRIOR_TICK + 1
+        for i in range(exps_until(TILES), TILES):
+            scale_minimum(i)
+            exp_stage(i)
         transpose_probs(first + 1)
-        normalise_and_store(first - 1, False)
-        for i in range(first + 1, TILES):
-            regroup_probs(i, nc.vector.tensor_copy)
-            quantise_probs(i - 1)
-            invert_sum(i)
-            if i + 1 < TILES:
-                transpose_probs(i + 1)
-            weighted_values(i - 1)
-            normalise_and_store(i - 1, False)
-        quantise_probs(TILES - 1)
-        weighted_values(TILES - 1)
-        normalise_and_store(TILES - 1, False)
+        multiplied, divided = first - MX_LAG, first - MX_LAG - 1
+        for i in range(first, TILES + 2):
+            if i < TILES:
+                regroup_probs(i, nc.vector.tensor_copy if (i - first) % TAIL_MOD else nc.scalar.copy)
+            if first <= i - 1 < TILES:
+                quantise_probs(i - 1)
+            if i < TILES:
+                invert_sum(i)
+            if i + 2 < TILES:
+                transpose_probs(i + 2)
+            while multiplied < min(i, TILES):
+                if multiplied - divided > 1:
+                    normalise_and_store(divided, False)
+                    divided += 1
+                weighted_values(multiplied)
+                multiplied += 1
+            while divided < min(i - 1, TILES):
+                normalise_and_store(divided, False)
+                divided += 1

@@ -28,18 +28,17 @@ BANK = 512
 
 LEAD = 14
 LOG_TICKS = 13
-WEIGHT_TICK = (3, 6)
 WLOAD = (1, 4)
-FEATURES_TICK = (2, 15)
-FEATURES_STEP = (1, 1)
-VALUES_TICK = (7, 20)
-KEYS_TICK = 8
+WEIGHT_TICK = (3, 6)
+FEATURES_TICK = (2, 13)
+VALUES_TICK = (7, 18)
+KEYS_TICK = 7
 KEYS_STEP = 2
-KEYS_VECTOR = 0
-FEATURES_VECTOR = (0, 1)
+EXP_RATE = (3, 2)
+LAST_OWN = TILES - LEAD + 2
 MX_LAG = 2
+TAIL_AHEAD = 2
 TAIL_MOD = 2
-LAST_PRIOR_TICK = TILES - LEAD
 
 
 def tile_pgwcrossattention_pa_t_kernel(tc, q, k, v_ret, pi_star, Wv, bv, gamma, out):
@@ -58,10 +57,14 @@ def tile_pgwcrossattention_pa_t_kernel(tc, q, k, v_ret, pi_star, Wv, bv, gamma, 
         keep = ctx.enter_context(tc.tile_pool(name="keep", bufs=2))
         work = ctx.enter_context(tc.tile_pool(name="work", bufs=2))
         psum = ctx.enter_context(tc.psum_pool(name="psum", bufs=2))
-        ctx.enter_context(tc.manual_schedule(engines={mybir.EngineType.Activation}))
+        ctx.enter_context(tc.manual_schedule())
 
         ident_f32 = const.tile([P, P], F32)
         make_identity(nc, ident_f32[:])
+        ident_bf16 = const.tile([P, P], BF16)
+        make_identity(nc, ident_bf16[:])
+        minus_one = const.tile([P, 2], F32)
+        nc.vector.memset(minus_one[:], -1.0)
         gamma_bf = const.tile([P, 1], BF16)
         bias_bf = const.tile([P, H], BF16)
         neg_gain = const.tile([P, 1], F32)
@@ -76,7 +79,7 @@ def tile_pgwcrossattention_pa_t_kernel(tc, q, k, v_ret, pi_star, Wv, bv, gamma, 
         wv_grouped, vr_grouped, vr_codes, vr_scales, v_grouped, v_codes, v_scales = {}, {}, {}, {}, {}, {}, {}
 
         def load_pi(j):
-            pi_raw[j] = raw.tile([P, 2, LK], BF16, name="pi_raw", bufs=3)
+            pi_raw[j] = raw.tile([P, 2, LK], BF16, name="pi_raw", tag="io", bufs=4)
             nc.sync.dma_start(out=pi_raw[j][:], in_=pi_view[:, 2 * j : 2 * j + 2, :])
 
         def load_q(j):
@@ -86,6 +89,17 @@ def tile_pgwcrossattention_pa_t_kernel(tc, q, k, v_ret, pi_star, Wv, bv, gamma, 
         def load_k(b, half):
             k_raw[b, half] = raw.tile([P, 4, H], BF16, name="k_raw", bufs=2)
             nc.sync.dma_start(out=k_raw[b, half][:], in_=k_view[:, b, 4 * half : 4 * half + 4, :])
+
+        def load_two_keys(j):
+            if j % 2 == 0:
+                k_raw[0, j // 2] = raw.tile([P, 4, H], BF16, name="k_raw", bufs=2)
+            n = 2 * (j % 2)
+            nc.sync.dma_start(out=k_raw[0, j // 2][:, n : n + 2, :], in_=k_view[:, 0, 2 * j : 2 * j + 2, :])
+
+        def load_one_pi(i):
+            if i % 2 == 0:
+                pi_raw[i // 2] = raw.tile([P, 2, LK], BF16, name="pi_raw", tag="io", bufs=4)
+            nc.sync.dma_start(out=pi_raw[i // 2][:, i % 2, :], in_=pi_view[:, i, :])
 
         def load_vr(b, j):
             vr_raw[b, j] = raw.tile([P, 2, DIN], BF16, name="vr_raw", tag="wide_raw", bufs=3)
@@ -107,11 +121,12 @@ def tile_pgwcrossattention_pa_t_kernel(tc, q, k, v_ret, pi_star, Wv, bv, gamma, 
             nc.scalar.activation(out=w[i][:], in_=w[i][:], func=ACT.Ln)
 
         def transpose_keys(b, j):
-            bank = psum.tile([P, 2, 2, P], F32, name="k_bank", tag="inputs")
-            for u in range(2):
-                for l in range(2):
-                    words = k_raw[b, j // 2][:, 2 * (j % 2) + l, :].bitcast(F32)
-                    nc.tensor.transpose(out=bank[:, u, l, :], in_=words[:, u * P : (u + 1) * P], identity=ident_f32[:])
+            bank = psum.tile([P, 2, 2, 2, P], BF16, name="k_bank", tag="inputs")
+            for l in range(2):
+                rows = k_raw[b, j // 2][:, 2 * (j % 2) + l, :].rearrange("p (u c y) -> p u y c", u=2, y=2)
+                for u in range(2):
+                    for y in range(2):
+                        nc.tensor.transpose(out=bank[:, u, y, l, :], in_=rows[:, u, y, :], identity=ident_bf16[:])
             k_bank[b, j] = bank
 
         def copy_keys(b, j, copy):
@@ -119,7 +134,7 @@ def tile_pgwcrossattention_pa_t_kernel(tc, q, k, v_ret, pi_star, Wv, bv, gamma, 
                 k_t[b] = keep.tile([P, 2, 2, LK], BF16, name="k_t")
             copy(
                 out=k_t[b][:, :, :, 2 * j * P : (2 * j + 2) * P],
-                in_=k_bank[b, j][:].rearrange("p u l k -> p u (l k)").bitcast(BF16).rearrange("p u (k y) -> p u y k", y=2),
+                in_=k_bank[b, j][:].rearrange("p u y l k -> p u y (l k)"),
             )
 
         def transpose_queries(j):
@@ -160,8 +175,10 @@ def tile_pgwcrossattention_pa_t_kernel(tc, q, k, v_ret, pi_star, Wv, bv, gamma, 
             nc.vector.tensor_reduce(out=w_min[i][:], in_=w[i][:], axis=AX.X, op=ALU.min)
 
         def scale_minimum(i):
-            exp_bias[i] = work.tile([P, 1], F32, name="exp_bias", bufs=4)
-            nc.scalar.activation(out=exp_bias[i][:], in_=w_min[i][:], func=ACT.Copy, scale=inv_sqrt_h)
+            exp_bias[i] = work.tile([P, 1], F32, name="exp_bias", bufs=8)
+            nc.gpsimd.tensor_scalar(
+                out=exp_bias[i][:], in0=w_min[i][:], scalar1=inv_sqrt_h, scalar2=0.0, op0=ALU.mult, op1=ALU.add
+            )
 
         def exp_stage(i):
             e[i] = keep.tile([P, LK], BF16, name="e", tag="w", bufs=TILES + 1)
@@ -173,7 +190,7 @@ def tile_pgwcrossattention_pa_t_kernel(tc, q, k, v_ret, pi_star, Wv, bv, gamma, 
             )
 
         def transpose_probs(i):
-            if i > LAST_PRIOR_TICK + 1:
+            if i >= LAST_OWN:
                 e_t[i] = psum.tile([P, PACK, P], F32, name="e_t_last", tag="z", bufs=3)
             else:
                 e_t[i] = psum.tile([P, PACK, P], F32, name="e_t", bufs=1)
@@ -182,7 +199,7 @@ def tile_pgwcrossattention_pa_t_kernel(tc, q, k, v_ret, pi_star, Wv, bv, gamma, 
                 nc.tensor.transpose(out=e_t[i][:, a, :], in_=words[:, a * P : (a + 1) * P], identity=ident_f32[:])
 
         def regroup_probs(i, copy):
-            e_grouped[i] = work.tile([P, 2, P, PACK], BF16, name="e_grouped", align_bytes=64)
+            e_grouped[i] = work.tile([P, 2, P, PACK], BF16, name="e_grouped", bufs=2, align_bytes=64)
             copy(out=e_grouped[i][:].bitcast(F32), in_=e_t[i][:].rearrange("p (c u) r -> p c r u", u=2))
 
         def quantise_probs(i):
@@ -196,7 +213,7 @@ def tile_pgwcrossattention_pa_t_kernel(tc, q, k, v_ret, pi_star, Wv, bv, gamma, 
         def invert_sum(i):
             if i % 2 == 0:
                 row_recip[i // 2] = work.tile([P, 2], F32, name="row_recip", bufs=4)
-                nc.vector.reciprocal(out=row_recip[i // 2][:], in_=row_sum[i // 2][:])
+                nc.gpsimd.tensor_tensor(out=row_recip[i // 2][:], in0=row_sum[i // 2][:], in1=minus_one[:], op=ALU.pow)
 
         def weighted_values(i):
             acc[i] = psum.tile([P, H], F32, name="acc", tag="mx")
@@ -212,7 +229,7 @@ def tile_pgwcrossattention_pa_t_kernel(tc, q, k, v_ret, pi_star, Wv, bv, gamma, 
                 )
 
         def normalise_and_store(i, on_vector):
-            o = work.tile([P, H], F32, name="o", bufs=4)
+            o = raw.tile([P, H], F32, name="o", tag="io", bufs=4)
             if on_vector:
                 nc.vector.tensor_scalar(out=o[:], in0=acc[i][:], scalar1=row_recip[i // 2][:, i % 2 : i % 2 + 1], scalar2=None, op0=ALU.mult)
             else:
@@ -296,43 +313,93 @@ def tile_pgwcrossattention_pa_t_kernel(tc, q, k, v_ret, pi_star, Wv, bv, gamma, 
             return max(0, min(TILES, -(-TILES * (h + 1) // LOG_TICKS)))
 
         def exps_until(h):
-            return max(0, min(TILES, h - 1, (3 * (h - LEAD + 2) + 1) // 2))
+            return max(0, min(TILES, h, -(-EXP_RATE[0] * (h - LEAD + 2) // EXP_RATE[1])))
 
         warm = const.tile([P, 1], F32)
         nc.vector.memset(warm[:], 1.0)
         nc.scalar.activation(out=warm[:], in_=warm[:], func=ACT.Ln)
-        load_pi(0)
-        load_k(0, 0)
+        load_two_keys(0)
+        load_one_pi(0)
         load_q(0)
-        load_k(0, 1)
+        load_two_keys(1)
+        load_one_pi(1)
+        load_two_keys(2)
+        load_two_keys(3)
+        nc.sync.dma_start(out=gamma_bf[:], in_=gamma.partition_broadcast(P))
         load_pi(1)
         load_q(1)
-        nc.sync.dma_start(out=gamma_bf[:], in_=gamma.partition_broadcast(P))
         load_pi(2)
         loaded = 3
         floor_stage(0)
         floor_stage(1)
-        log_stage(0)
         transpose_keys(0, 0)
-        transpose_keys(0, 1)
-        copy_keys(0, 0, nc.vector.tensor_copy)
-        copy_keys(0, 1, nc.vector.tensor_copy)
+        copy_keys(0, 0, nc.scalar.copy)
         transpose_queries(0)
         copy_queries(0, nc.vector.tensor_copy)
+        log_stage(0)
+        transpose_keys(0, 1)
+        copy_keys(0, 1, nc.scalar.copy)
         log_stage(1)
         transpose_keys(0, 2)
+        copy_keys(0, 2, nc.vector.tensor_copy)
         transpose_keys(0, 3)
-        copy_keys(0, 2, nc.scalar.copy)
-        copy_keys(0, 3, nc.scalar.copy)
+        copy_keys(0, 3, nc.vector.tensor_copy)
         nc.vector.tensor_scalar(out=neg_gain[:], in0=gamma_bf[:], scalar1=-math.sqrt(H), scalar2=None, op0=ALU.mult)
 
         for h in range(TILES + 1):
             tick = h - LEAD
-            cur, mul, div, following, new = tick, tick - MX_LAG, tick - MX_LAG - 1, tick + 1, h
-            exps = list(range(exps_until(h - 1), exps_until(h)))
-            logs = list(range(max(2, logs_until(h - 1)), logs_until(h)))
+            cur, mul, div, following = tick, tick - MX_LAG, tick - MX_LAG - 1, tick + 1
+            exps = range(exps_until(h - 1), exps_until(h))
+            logs = range(max(2, logs_until(h - 1)), logs_until(h))
+            n, r = divmod(h - KEYS_TICK, KEYS_STEP)
+            if r == 0 and 0 <= n < 4:
+                transpose_keys(1, n)
+            for i in exps[:1]:
+                scale_minimum(i)
+                exp_stage(i)
+            if h >= 1:
+                add_prior(h - 1)
+            if div >= 0:
+                normalise_and_store(div, False)
+            if h < TILES:
+                scores(h, 0)
+            if cur >= 0:
+                invert_sum(cur)
+            if h in WEIGHT_TICK:
+                group_weights(WEIGHT_TICK.index(h))
             for i in logs:
                 floor_stage(i)
+            for b in range(B):
+                if h - 2 - VALUES_TICK[b] in (3, 7):
+                    quantise_values(b, (h - 2 - VALUES_TICK[b]) // 4)
+            if h < TILES:
+                scores(h, 1)
+            if h % 2 == 1 and (h + 1) // 2 < NB:
+                copy_queries((h + 1) // 2, nc.vector.tensor_copy)
+            if cur >= 0:
+                regroup_probs(cur, nc.scalar.copy)
+            for b in range(B):
+                if 0 <= h - 1 - VALUES_TICK[b] < 8:
+                    add_bias(b, h - 1 - VALUES_TICK[b])
+            for i in logs[:1]:
+                log_stage(i)
+            for i in exps[1:]:
+                scale_minimum(i)
+                exp_stage(i)
+            for b in range(B):
+                n = h - 2 - FEATURES_TICK[b]
+                if n % 2 == 1 and 0 <= n < 8:
+                    quantise_features(b, n // 2)
+            if h - 1 in WEIGHT_TICK:
+                quantise_weights(WEIGHT_TICK.index(h - 1))
+            for b in range(B):
+                if 0 <= h - VALUES_TICK[b] < 8:
+                    project_values(b, h - VALUES_TICK[b], "mx")
+            if mul >= 0:
+                weighted_values(mul)
+            n, r = divmod(h - 1 - KEYS_TICK, KEYS_STEP)
+            if r == 0 and 0 <= n < 4:
+                copy_keys(1, n, nc.scalar.copy)
             while loaded < min(NB, logs_until(h) // 2 + 3):
                 load_pi(loaded)
                 loaded += 1
@@ -348,79 +415,31 @@ def tile_pgwcrossattention_pa_t_kernel(tc, q, k, v_ret, pi_star, Wv, bv, gamma, 
                     load_vr(b, n // 2)
             if h + 3 - KEYS_TICK in (0, 1):
                 load_k(1, h + 3 - KEYS_TICK)
-            if new < TILES:
-                scores(new, 0)
-            for i in logs[:1]:
-                log_stage(i)
-            for i in exps[:1]:
-                scale_minimum(i)
-                exp_stage(i)
-            if cur >= 0:
-                regroup_probs(cur, nc.scalar.copy)
-            if div >= 0:
-                normalise_and_store(div, False)
-            if new >= 1:
-                add_prior(new - 1)
-            if h % 2 == 1 and (h + 1) // 2 < NB:
-                copy_queries((h + 1) // 2, nc.vector.tensor_copy)
-            if h - 1 in WEIGHT_TICK:
-                quantise_weights(WEIGHT_TICK.index(h - 1))
-            for b in range(B):
-                n = h - 2 - FEATURES_TICK[b]
-                if n % 2 == 1 and 0 <= n < 8:
-                    quantise_features(b, n // 2)
-            for b in range(B):
-                n = h - 2 - VALUES_TICK[b]
-                if n in (3, 7):
-                    quantise_values(b, n // 4)
-            if new >= 1:
-                row_minimum(new - 1)
-            n, r = divmod(h - 1 - KEYS_TICK, KEYS_STEP)
-            if r == 0 and 0 <= n < 4:
-                copy_keys(1, n, nc.vector.tensor_copy if n < KEYS_VECTOR else nc.scalar.copy)
+            if h % 2 == 0 and h // 2 + 1 < NB:
+                transpose_queries(h // 2 + 1)
             for b in range(B):
                 n = h - 1 - FEATURES_TICK[b]
                 if 0 <= n < 8:
-                    copy_features(b, n, nc.vector.tensor_copy if n % 2 < FEATURES_VECTOR[b] else nc.scalar.copy)
-            for b in range(B):
-                n = h - 1 - VALUES_TICK[b]
-                if 0 <= n < 8:
-                    add_bias(b, n)
-            if cur >= 0:
-                quantise_probs(cur)
-                invert_sum(cur)
-            if h in WEIGHT_TICK:
-                group_weights(WEIGHT_TICK.index(h))
+                    copy_features(b, n, nc.vector.tensor_copy if b == 1 and n % 2 == 0 else nc.scalar.copy)
             for i in logs[1:]:
                 log_stage(i)
-            for i in exps[1:]:
-                scale_minimum(i)
-                exp_stage(i)
-            if mul >= 0:
-                weighted_values(mul)
-            for b in range(B):
-                n = h - VALUES_TICK[b]
-                if 0 <= n < 8:
-                    project_values(b, n, "mx")
-            if new < TILES:
-                scores(new, 1)
+            if following >= 0:
+                transpose_probs(following)
+            if h >= 1:
+                row_minimum(h - 1)
             for b in range(B):
                 n = h - FEATURES_TICK[b]
                 if 0 <= n < 8:
                     transpose_features(b, n, "inputs" if b else "mx")
-            if h % 2 == 0 and h // 2 + 1 < NB:
-                transpose_queries(h // 2 + 1)
-            n, r = divmod(h - KEYS_TICK, KEYS_STEP)
-            if r == 0 and 0 <= n < 4:
-                transpose_keys(1, n)
-            if following >= 0:
-                transpose_probs(following)
+            if cur >= 0:
+                quantise_probs(cur)
 
-        first = LAST_PRIOR_TICK + 1
+        first = TILES - LEAD + 1
         for i in range(exps_until(TILES), TILES):
             scale_minimum(i)
             exp_stage(i)
-        transpose_probs(first + 1)
+        for i in range(first + 1, first + TAIL_AHEAD):
+            transpose_probs(i)
         multiplied, divided = first - MX_LAG, first - MX_LAG - 1
         for i in range(first, TILES + 2):
             if i < TILES:
@@ -429,8 +448,8 @@ def tile_pgwcrossattention_pa_t_kernel(tc, q, k, v_ret, pi_star, Wv, bv, gamma, 
                 quantise_probs(i - 1)
             if i < TILES:
                 invert_sum(i)
-            if i + 2 < TILES:
-                transpose_probs(i + 2)
+            if i + TAIL_AHEAD < TILES:
+                transpose_probs(i + TAIL_AHEAD)
             while multiplied < min(i, TILES):
                 if multiplied - divided > 1:
                     normalise_and_store(divided, False)

@@ -26,18 +26,19 @@ KEY_TILES = LK // P
 BANK = 512
 
 
-LEAD = 14
+LEAD = 15
 LOG_TICKS = 13
-WLOAD = (1, 4)
+WLOAD = (0, 4)
 WEIGHT_TICK = (3, 6)
 FEATURES_TICK = (2, 13)
 VALUES_TICK = (7, 18)
-KEYS_TICK = 7
+VALUES_STEP = (1, 1)
+KEYS_TICK = 4
 KEYS_STEP = 2
-EXP_RATE = (3, 2)
+EXP_RATE = (7, 4)
 LAST_OWN = TILES - LEAD + 2
-MX_LAG = 2
-TAIL_AHEAD = 2
+MX_LAG = 1
+GROUP = 2
 TAIL_MOD = 2
 
 
@@ -61,8 +62,6 @@ def tile_pgwcrossattention_pa_t_kernel(tc, q, k, v_ret, pi_star, Wv, bv, gamma, 
 
         ident_f32 = const.tile([P, P], F32)
         make_identity(nc, ident_f32[:])
-        ident_bf16 = const.tile([P, P], BF16)
-        make_identity(nc, ident_bf16[:])
         minus_one = const.tile([P, 2], F32)
         nc.vector.memset(minus_one[:], -1.0)
         gamma_bf = const.tile([P, 1], BF16)
@@ -121,12 +120,11 @@ def tile_pgwcrossattention_pa_t_kernel(tc, q, k, v_ret, pi_star, Wv, bv, gamma, 
             nc.scalar.activation(out=w[i][:], in_=w[i][:], func=ACT.Ln)
 
         def transpose_keys(b, j):
-            bank = psum.tile([P, 2, 2, 2, P], BF16, name="k_bank", tag="inputs")
-            for l in range(2):
-                rows = k_raw[b, j // 2][:, 2 * (j % 2) + l, :].rearrange("p (u c y) -> p u y c", u=2, y=2)
-                for u in range(2):
-                    for y in range(2):
-                        nc.tensor.transpose(out=bank[:, u, y, l, :], in_=rows[:, u, y, :], identity=ident_bf16[:])
+            bank = psum.tile([P, 2, 2, P], F32, name="k_bank", tag="inputs")
+            for u in range(2):
+                for l in range(2):
+                    words = k_raw[b, j // 2][:, 2 * (j % 2) + l, :].bitcast(F32)
+                    nc.tensor.transpose(out=bank[:, u, l, :], in_=words[:, u * P : (u + 1) * P], identity=ident_f32[:])
             k_bank[b, j] = bank
 
         def copy_keys(b, j, copy):
@@ -134,7 +132,7 @@ def tile_pgwcrossattention_pa_t_kernel(tc, q, k, v_ret, pi_star, Wv, bv, gamma, 
                 k_t[b] = keep.tile([P, 2, 2, LK], BF16, name="k_t")
             copy(
                 out=k_t[b][:, :, :, 2 * j * P : (2 * j + 2) * P],
-                in_=k_bank[b, j][:].rearrange("p u y l k -> p u y (l k)"),
+                in_=k_bank[b, j][:].rearrange("p u l k -> p u (l k)").bitcast(BF16).rearrange("p u (k y) -> p u y k", y=2),
             )
 
         def transpose_queries(j):
@@ -191,7 +189,7 @@ def tile_pgwcrossattention_pa_t_kernel(tc, q, k, v_ret, pi_star, Wv, bv, gamma, 
 
         def transpose_probs(i):
             if i >= LAST_OWN:
-                e_t[i] = psum.tile([P, PACK, P], F32, name="e_t_last", tag="z", bufs=3)
+                e_t[i] = psum.tile([P, PACK, P], F32, name="e_t_last", tag="z", bufs=3) if i % 2 else psum.tile([P, PACK, P], F32, name="e_t_last", tag="inputs")
             else:
                 e_t[i] = psum.tile([P, PACK, P], F32, name="e_t", bufs=1)
             words = e[i][:].bitcast(F32)
@@ -312,8 +310,11 @@ def tile_pgwcrossattention_pa_t_kernel(tc, q, k, v_ret, pi_star, Wv, bv, gamma, 
         def logs_until(h):
             return max(0, min(TILES, -(-TILES * (h + 1) // LOG_TICKS)))
 
+        def value_tick(b, n):
+            return VALUES_TICK[b] + n // VALUES_STEP[b]
+
         def exps_until(h):
-            return max(0, min(TILES, h, -(-EXP_RATE[0] * (h - LEAD + 2) // EXP_RATE[1])))
+            return max(0, min(TILES, h - 1, -(-EXP_RATE[0] * (h - LEAD + 2) // EXP_RATE[1])))
 
         warm = const.tile([P, 1], F32)
         nc.vector.memset(warm[:], 1.0)
@@ -333,17 +334,17 @@ def tile_pgwcrossattention_pa_t_kernel(tc, q, k, v_ret, pi_star, Wv, bv, gamma, 
         floor_stage(0)
         floor_stage(1)
         transpose_keys(0, 0)
-        copy_keys(0, 0, nc.scalar.copy)
+        copy_keys(0, 0, nc.vector.tensor_copy)
         transpose_queries(0)
         copy_queries(0, nc.vector.tensor_copy)
         log_stage(0)
         transpose_keys(0, 1)
-        copy_keys(0, 1, nc.scalar.copy)
+        copy_keys(0, 1, nc.vector.tensor_copy)
         log_stage(1)
         transpose_keys(0, 2)
         copy_keys(0, 2, nc.vector.tensor_copy)
         transpose_keys(0, 3)
-        copy_keys(0, 3, nc.vector.tensor_copy)
+        copy_keys(0, 3, nc.scalar.copy)
         nc.vector.tensor_scalar(out=neg_gain[:], in0=gamma_bf[:], scalar1=-math.sqrt(H), scalar2=None, op0=ALU.mult)
 
         for h in range(TILES + 1):
@@ -351,55 +352,35 @@ def tile_pgwcrossattention_pa_t_kernel(tc, q, k, v_ret, pi_star, Wv, bv, gamma, 
             cur, mul, div, following = tick, tick - MX_LAG, tick - MX_LAG - 1, tick + 1
             exps = range(exps_until(h - 1), exps_until(h))
             logs = range(max(2, logs_until(h - 1)), logs_until(h))
-            n, r = divmod(h - KEYS_TICK, KEYS_STEP)
-            if r == 0 and 0 <= n < 4:
-                transpose_keys(1, n)
+            for i in logs:
+                floor_stage(i)
             for i in exps[:1]:
                 scale_minimum(i)
                 exp_stage(i)
             if h >= 1:
                 add_prior(h - 1)
-            if div >= 0:
-                normalise_and_store(div, False)
-            if h < TILES:
-                scores(h, 0)
-            if cur >= 0:
-                invert_sum(cur)
+            n, r = divmod(h - 1 - KEYS_TICK, KEYS_STEP)
+            if r == 0 and 0 <= n < 4:
+                copy_keys(1, n, nc.scalar.copy)
+            for b in range(B):
+                for c in range(2):
+                    if h == value_tick(b, 4 * c + 3) + 2:
+                        quantise_values(b, c)
+            if h - 1 in WEIGHT_TICK:
+                quantise_weights(WEIGHT_TICK.index(h - 1))
+            n, r = divmod(h - KEYS_TICK, KEYS_STEP)
+            if r == 0 and 0 <= n < 4:
+                transpose_keys(1, n)
             if h in WEIGHT_TICK:
                 group_weights(WEIGHT_TICK.index(h))
-            for i in logs:
-                floor_stage(i)
-            for b in range(B):
-                if h - 2 - VALUES_TICK[b] in (3, 7):
-                    quantise_values(b, (h - 2 - VALUES_TICK[b]) // 4)
-            if h < TILES:
-                scores(h, 1)
-            if h % 2 == 1 and (h + 1) // 2 < NB:
-                copy_queries((h + 1) // 2, nc.vector.tensor_copy)
-            if cur >= 0:
-                regroup_probs(cur, nc.scalar.copy)
-            for b in range(B):
-                if 0 <= h - 1 - VALUES_TICK[b] < 8:
-                    add_bias(b, h - 1 - VALUES_TICK[b])
-            for i in logs[:1]:
-                log_stage(i)
-            for i in exps[1:]:
-                scale_minimum(i)
-                exp_stage(i)
             for b in range(B):
                 n = h - 2 - FEATURES_TICK[b]
                 if n % 2 == 1 and 0 <= n < 8:
                     quantise_features(b, n // 2)
-            if h - 1 in WEIGHT_TICK:
-                quantise_weights(WEIGHT_TICK.index(h - 1))
-            for b in range(B):
-                if 0 <= h - VALUES_TICK[b] < 8:
-                    project_values(b, h - VALUES_TICK[b], "mx")
-            if mul >= 0:
-                weighted_values(mul)
-            n, r = divmod(h - 1 - KEYS_TICK, KEYS_STEP)
-            if r == 0 and 0 <= n < 4:
-                copy_keys(1, n, nc.scalar.copy)
+            if div >= 0:
+                normalise_and_store(div, False)
+            if h < TILES:
+                scores(h, 0)
             while loaded < min(NB, logs_until(h) // 2 + 3):
                 load_pi(loaded)
                 loaded += 1
@@ -415,47 +396,71 @@ def tile_pgwcrossattention_pa_t_kernel(tc, q, k, v_ret, pi_star, Wv, bv, gamma, 
                     load_vr(b, n // 2)
             if h + 3 - KEYS_TICK in (0, 1):
                 load_k(1, h + 3 - KEYS_TICK)
-            if h % 2 == 0 and h // 2 + 1 < NB:
-                transpose_queries(h // 2 + 1)
+            if h < TILES:
+                scores(h, 1)
             for b in range(B):
                 n = h - 1 - FEATURES_TICK[b]
                 if 0 <= n < 8:
                     copy_features(b, n, nc.vector.tensor_copy if b == 1 and n % 2 == 0 else nc.scalar.copy)
-            for i in logs[1:]:
-                log_stage(i)
+            if cur >= 0:
+                regroup_probs(cur, nc.scalar.copy)
+            for b in range(B):
+                for n in range(8):
+                    if h == value_tick(b, n) + 1:
+                        add_bias(b, n)
+            for b in range(B):
+                for n in range(8):
+                    if h == value_tick(b, n):
+                        project_values(b, n, "mx")
+            if h % 2 == 1 and (h + 1) // 2 < NB:
+                copy_queries((h + 1) // 2, nc.vector.tensor_copy if h < LEAD else nc.scalar.copy)
+            if mul >= 0:
+                weighted_values(mul)
+            if h % 2 == 0 and h // 2 + 1 < NB:
+                transpose_queries(h // 2 + 1)
             if following >= 0:
                 transpose_probs(following)
+            for i in exps[1:]:
+                scale_minimum(i)
+                exp_stage(i)
+            for i in logs[:1]:
+                log_stage(i)
             if h >= 1:
                 row_minimum(h - 1)
+            if cur >= 0:
+                invert_sum(cur)
             for b in range(B):
                 n = h - FEATURES_TICK[b]
                 if 0 <= n < 8:
                     transpose_features(b, n, "inputs" if b else "mx")
             if cur >= 0:
                 quantise_probs(cur)
+            for i in logs[1:]:
+                log_stage(i)
 
         first = TILES - LEAD + 1
         for i in range(exps_until(TILES), TILES):
             scale_minimum(i)
             exp_stage(i)
-        for i in range(first + 1, first + TAIL_AHEAD):
-            transpose_probs(i)
-        multiplied, divided = first - MX_LAG, first - MX_LAG - 1
-        for i in range(first, TILES + 2):
-            if i < TILES:
-                regroup_probs(i, nc.vector.tensor_copy if (i - first) % TAIL_MOD else nc.scalar.copy)
-            if first <= i - 1 < TILES:
-                quantise_probs(i - 1)
-            if i < TILES:
+        groups = [[first]] + [list(range(i, min(i + GROUP, TILES))) for i in range(first + 1, TILES, GROUP)]
+        waiting = list(range(first - MX_LAG, first))
+        divided = first - MX_LAG - 1
+        for n in range(len(groups) + 1):
+            current = groups[n] if n < len(groups) else []
+            for i in current:
+                regroup_probs(i, nc.scalar.copy if i % TAIL_MOD == 0 else nc.vector.tensor_copy)
                 invert_sum(i)
-            if i + TAIL_AHEAD < TILES:
-                transpose_probs(i + TAIL_AHEAD)
-            while multiplied < min(i, TILES):
-                if multiplied - divided > 1:
+            for i in groups[n + 1] if n + 1 < len(groups) else []:
+                transpose_probs(i)
+            for i in waiting:
+                if i - divided > 1:
                     normalise_and_store(divided, False)
                     divided += 1
-                weighted_values(multiplied)
-                multiplied += 1
-            while divided < min(i - 1, TILES):
+                weighted_values(i)
+            for i in current:
+                quantise_probs(i)
+            while divided < (waiting[-1] if waiting else TILES):
                 normalise_and_store(divided, False)
                 divided += 1
+            waiting = current
+        normalise_and_store(TILES - 1, False)

@@ -27,19 +27,20 @@ BANK = 512
 
 
 LEAD = 15
-LOG_TICKS = 13
-WLOAD = (0, 4)
-WEIGHT_TICK = (3, 6)
+LOG_TICKS = 15
+WLOAD = (0, 1)
+WEIGHT_TICK = (2, 6)
 FEATURES_TICK = (2, 13)
-VALUES_TICK = (7, 18)
+VALUES_TICK = (7, 19)
 VALUES_STEP = (1, 1)
-KEYS_TICK = 4
+KEYS_TICK = 3
 KEYS_STEP = 2
 EXP_RATE = (7, 4)
 LAST_OWN = TILES - LEAD + 2
 MX_LAG = 1
 GROUP = 2
-TAIL_MOD = 2
+OUTSTANDING = 1
+TAIL_MOD = 5
 
 
 def tile_pgwcrossattention_pa_t_kernel(tc, q, k, v_ret, pi_star, Wv, bv, gamma, out):
@@ -62,6 +63,8 @@ def tile_pgwcrossattention_pa_t_kernel(tc, q, k, v_ret, pi_star, Wv, bv, gamma, 
 
         ident_f32 = const.tile([P, P], F32)
         make_identity(nc, ident_f32[:])
+        ident_bf16 = const.tile([P, P], BF16)
+        make_identity(nc, ident_bf16[:])
         minus_one = const.tile([P, 2], F32)
         nc.vector.memset(minus_one[:], -1.0)
         gamma_bf = const.tile([P, 1], BF16)
@@ -120,11 +123,12 @@ def tile_pgwcrossattention_pa_t_kernel(tc, q, k, v_ret, pi_star, Wv, bv, gamma, 
             nc.scalar.activation(out=w[i][:], in_=w[i][:], func=ACT.Ln)
 
         def transpose_keys(b, j):
-            bank = psum.tile([P, 2, 2, P], F32, name="k_bank", tag="inputs")
-            for u in range(2):
-                for l in range(2):
-                    words = k_raw[b, j // 2][:, 2 * (j % 2) + l, :].bitcast(F32)
-                    nc.tensor.transpose(out=bank[:, u, l, :], in_=words[:, u * P : (u + 1) * P], identity=ident_f32[:])
+            bank = psum.tile([P, 2, 2, 2, P], BF16, name="k_bank", tag="inputs")
+            for l in range(2):
+                rows = k_raw[b, j // 2][:, 2 * (j % 2) + l, :].rearrange("p (u c y) -> p u y c", u=2, y=2)
+                for u in range(2):
+                    for y in range(2):
+                        nc.tensor.transpose(out=bank[:, u, y, l, :], in_=rows[:, u, y, :], identity=ident_bf16[:])
             k_bank[b, j] = bank
 
         def copy_keys(b, j, copy):
@@ -132,7 +136,7 @@ def tile_pgwcrossattention_pa_t_kernel(tc, q, k, v_ret, pi_star, Wv, bv, gamma, 
                 k_t[b] = keep.tile([P, 2, 2, LK], BF16, name="k_t")
             copy(
                 out=k_t[b][:, :, :, 2 * j * P : (2 * j + 2) * P],
-                in_=k_bank[b, j][:].rearrange("p u l k -> p u (l k)").bitcast(BF16).rearrange("p u (k y) -> p u y k", y=2),
+                in_=k_bank[b, j][:].rearrange("p u y l k -> p u y (l k)"),
             )
 
         def transpose_queries(j):
@@ -214,7 +218,10 @@ def tile_pgwcrossattention_pa_t_kernel(tc, q, k, v_ret, pi_star, Wv, bv, gamma, 
                 nc.gpsimd.tensor_tensor(out=row_recip[i // 2][:], in0=row_sum[i // 2][:], in1=minus_one[:], op=ALU.pow)
 
         def weighted_values(i):
-            acc[i] = psum.tile([P, H], F32, name="acc", tag="mx")
+            if i > LAST_OWN and i % 3 == 0:
+                acc[i] = psum.tile([P, H], F32, name="acc_last", tag="e_t", bufs=1)
+            else:
+                acc[i] = psum.tile([P, H], F32, name="acc", tag="mx")
             for c in range(2):
                 nc.tensor.matmul_mx(
                     out=acc[i][:],
@@ -227,7 +234,10 @@ def tile_pgwcrossattention_pa_t_kernel(tc, q, k, v_ret, pi_star, Wv, bv, gamma, 
                 )
 
         def normalise_and_store(i, on_vector):
-            o = raw.tile([P, H], F32, name="o", tag="io", bufs=4)
+            if i >= LAST_OWN:
+                o = keep.tile([P, H], F32, name="o_last", tag="w", bufs=TILES + 1)
+            else:
+                o = raw.tile([P, H], F32, name="o", tag="io", bufs=4)
             if on_vector:
                 nc.vector.tensor_scalar(out=o[:], in0=acc[i][:], scalar1=row_recip[i // 2][:, i % 2 : i % 2 + 1], scalar2=None, op0=ALU.mult)
             else:
@@ -339,12 +349,12 @@ def tile_pgwcrossattention_pa_t_kernel(tc, q, k, v_ret, pi_star, Wv, bv, gamma, 
         copy_queries(0, nc.vector.tensor_copy)
         log_stage(0)
         transpose_keys(0, 1)
-        copy_keys(0, 1, nc.vector.tensor_copy)
+        copy_keys(0, 1, nc.scalar.copy)
         log_stage(1)
         transpose_keys(0, 2)
-        copy_keys(0, 2, nc.vector.tensor_copy)
+        copy_keys(0, 2, nc.scalar.copy)
         transpose_keys(0, 3)
-        copy_keys(0, 3, nc.scalar.copy)
+        copy_keys(0, 3, nc.vector.tensor_copy)
         nc.vector.tensor_scalar(out=neg_gain[:], in0=gamma_bf[:], scalar1=-math.sqrt(H), scalar2=None, op0=ALU.mult)
 
         for h in range(TILES + 1):
@@ -352,35 +362,71 @@ def tile_pgwcrossattention_pa_t_kernel(tc, q, k, v_ret, pi_star, Wv, bv, gamma, 
             cur, mul, div, following = tick, tick - MX_LAG, tick - MX_LAG - 1, tick + 1
             exps = range(exps_until(h - 1), exps_until(h))
             logs = range(max(2, logs_until(h - 1)), logs_until(h))
-            for i in logs:
-                floor_stage(i)
-            for i in exps[:1]:
-                scale_minimum(i)
-                exp_stage(i)
-            if h >= 1:
-                add_prior(h - 1)
+            if h < TILES:
+                scores(h, 0)
             n, r = divmod(h - 1 - KEYS_TICK, KEYS_STEP)
             if r == 0 and 0 <= n < 4:
                 copy_keys(1, n, nc.scalar.copy)
+            if div >= 0:
+                normalise_and_store(div, False)
+            n, r = divmod(h - KEYS_TICK, KEYS_STEP)
+            if r == 0 and 0 <= n < 4:
+                transpose_keys(1, n)
+            if cur >= 0:
+                regroup_probs(cur, nc.scalar.copy)
+            if h >= 1:
+                add_prior(h - 1)
+            if cur >= 0:
+                invert_sum(cur)
             for b in range(B):
                 for c in range(2):
                     if h == value_tick(b, 4 * c + 3) + 2:
                         quantise_values(b, c)
-            if h - 1 in WEIGHT_TICK:
-                quantise_weights(WEIGHT_TICK.index(h - 1))
-            n, r = divmod(h - KEYS_TICK, KEYS_STEP)
-            if r == 0 and 0 <= n < 4:
-                transpose_keys(1, n)
+            for i in logs:
+                floor_stage(i)
+            for i in logs[:1]:
+                log_stage(i)
+            if mul >= 0:
+                weighted_values(mul)
             if h in WEIGHT_TICK:
                 group_weights(WEIGHT_TICK.index(h))
+            if h - 1 in WEIGHT_TICK:
+                quantise_weights(WEIGHT_TICK.index(h - 1))
             for b in range(B):
                 n = h - 2 - FEATURES_TICK[b]
                 if n % 2 == 1 and 0 <= n < 8:
                     quantise_features(b, n // 2)
-            if div >= 0:
-                normalise_and_store(div, False)
+            for b in range(B):
+                for n in range(8):
+                    if h == value_tick(b, n) + 1:
+                        add_bias(b, n)
             if h < TILES:
-                scores(h, 0)
+                scores(h, 1)
+            if h % 2 == 1 and (h + 1) // 2 < NB:
+                copy_queries((h + 1) // 2, nc.vector.tensor_copy if h < LEAD else nc.scalar.copy)
+            for b in range(B):
+                for n in range(8):
+                    if h == value_tick(b, n):
+                        project_values(b, n, "mx")
+            for i in logs[1:]:
+                log_stage(i)
+            for i in exps[:1]:
+                scale_minimum(i)
+                exp_stage(i)
+            for b in range(B):
+                n = h - 1 - FEATURES_TICK[b]
+                if 0 <= n < 8:
+                    copy_features(b, n, nc.vector.tensor_copy if b == 1 and n % 2 == 0 else nc.scalar.copy)
+            if following >= 0:
+                transpose_probs(following)
+            if h % 2 == 0 and h // 2 + 1 < NB:
+                transpose_queries(h // 2 + 1)
+            for b in range(B):
+                n = h - FEATURES_TICK[b]
+                if 0 <= n < 8:
+                    transpose_features(b, n, "inputs" if b else "mx")
+            if h >= 1:
+                row_minimum(h - 1)
             while loaded < min(NB, logs_until(h) // 2 + 3):
                 load_pi(loaded)
                 loaded += 1
@@ -396,47 +442,11 @@ def tile_pgwcrossattention_pa_t_kernel(tc, q, k, v_ret, pi_star, Wv, bv, gamma, 
                     load_vr(b, n // 2)
             if h + 3 - KEYS_TICK in (0, 1):
                 load_k(1, h + 3 - KEYS_TICK)
-            if h < TILES:
-                scores(h, 1)
-            for b in range(B):
-                n = h - 1 - FEATURES_TICK[b]
-                if 0 <= n < 8:
-                    copy_features(b, n, nc.vector.tensor_copy if b == 1 and n % 2 == 0 else nc.scalar.copy)
             if cur >= 0:
-                regroup_probs(cur, nc.scalar.copy)
-            for b in range(B):
-                for n in range(8):
-                    if h == value_tick(b, n) + 1:
-                        add_bias(b, n)
-            for b in range(B):
-                for n in range(8):
-                    if h == value_tick(b, n):
-                        project_values(b, n, "mx")
-            if h % 2 == 1 and (h + 1) // 2 < NB:
-                copy_queries((h + 1) // 2, nc.vector.tensor_copy if h < LEAD else nc.scalar.copy)
-            if mul >= 0:
-                weighted_values(mul)
-            if h % 2 == 0 and h // 2 + 1 < NB:
-                transpose_queries(h // 2 + 1)
-            if following >= 0:
-                transpose_probs(following)
+                quantise_probs(cur)
             for i in exps[1:]:
                 scale_minimum(i)
                 exp_stage(i)
-            for i in logs[:1]:
-                log_stage(i)
-            if h >= 1:
-                row_minimum(h - 1)
-            if cur >= 0:
-                invert_sum(cur)
-            for b in range(B):
-                n = h - FEATURES_TICK[b]
-                if 0 <= n < 8:
-                    transpose_features(b, n, "inputs" if b else "mx")
-            if cur >= 0:
-                quantise_probs(cur)
-            for i in logs[1:]:
-                log_stage(i)
 
         first = TILES - LEAD + 1
         for i in range(exps_until(TILES), TILES):
@@ -453,7 +463,7 @@ def tile_pgwcrossattention_pa_t_kernel(tc, q, k, v_ret, pi_star, Wv, bv, gamma, 
             for i in groups[n + 1] if n + 1 < len(groups) else []:
                 transpose_probs(i)
             for i in waiting:
-                if i - divided > 1:
+                if i - divided > OUTSTANDING:
                     normalise_and_store(divided, False)
                     divided += 1
                 weighted_values(i)

@@ -27,10 +27,10 @@ BANK = 512
 
 
 LEAD = 15
-LOG_TICKS = 15
-WLOAD = (0, 1)
+LOG_TICKS = 14
+WLOAD = (0, 4)
 WEIGHT_TICK = (2, 6)
-FEATURES_TICK = (2, 13)
+FEATURES_TICK = (2, 14)
 VALUES_TICK = (7, 19)
 VALUES_STEP = (1, 1)
 KEYS_TICK = 3
@@ -40,6 +40,8 @@ LAST_OWN = TILES - LEAD + 2
 MX_LAG = 1
 GROUP = 2
 OUTSTANDING = 1
+PARTED = (False, True)
+QLAG = 0
 TAIL_MOD = 5
 
 
@@ -63,8 +65,6 @@ def tile_pgwcrossattention_pa_t_kernel(tc, q, k, v_ret, pi_star, Wv, bv, gamma, 
 
         ident_f32 = const.tile([P, P], F32)
         make_identity(nc, ident_f32[:])
-        ident_bf16 = const.tile([P, P], BF16)
-        make_identity(nc, ident_bf16[:])
         minus_one = const.tile([P, 2], F32)
         nc.vector.memset(minus_one[:], -1.0)
         gamma_bf = const.tile([P, 1], BF16)
@@ -123,21 +123,23 @@ def tile_pgwcrossattention_pa_t_kernel(tc, q, k, v_ret, pi_star, Wv, bv, gamma, 
             nc.scalar.activation(out=w[i][:], in_=w[i][:], func=ACT.Ln)
 
         def transpose_keys(b, j):
-            bank = psum.tile([P, 2, 2, 2, P], BF16, name="k_bank", tag="inputs")
-            for l in range(2):
-                rows = k_raw[b, j // 2][:, 2 * (j % 2) + l, :].rearrange("p (u c y) -> p u y c", u=2, y=2)
-                for u in range(2):
-                    for y in range(2):
-                        nc.tensor.transpose(out=bank[:, u, y, l, :], in_=rows[:, u, y, :], identity=ident_bf16[:])
+            bank = psum.tile([P, 2, 2, P], F32, name="k_bank", tag="inputs")
+            for u in range(2):
+                for l in range(2):
+                    words = k_raw[b, j // 2][:, 2 * (j % 2) + l, :].bitcast(F32)
+                    nc.tensor.transpose(out=bank[:, u, l, :], in_=words[:, u * P : (u + 1) * P], identity=ident_f32[:])
             k_bank[b, j] = bank
 
         def copy_keys(b, j, copy):
             if j == 0:
-                k_t[b] = keep.tile([P, 2, 2, LK], BF16, name="k_t")
-            copy(
-                out=k_t[b][:, :, :, 2 * j * P : (2 * j + 2) * P],
-                in_=k_bank[b, j][:].rearrange("p u y l k -> p u y (l k)"),
-            )
+                k_t[b] = keep.tile([P, 2, LK], F32, name="k_t") if not PARTED[b] else keep.tile([P, 2, 2, LK], BF16, name="k_t")
+            if PARTED[b]:
+                copy(
+                    out=k_t[b][:, :, :, 2 * j * P : (2 * j + 2) * P],
+                    in_=k_bank[b, j][:].rearrange("p u l k -> p u (l k)").bitcast(BF16).rearrange("p u (k y) -> p u y k", y=2),
+                )
+            else:
+                copy(out=k_t[b][:, :, 2 * j * P : (2 * j + 2) * P], in_=k_bank[b, j][:].rearrange("p u l k -> p u (l k)"))
 
         def transpose_queries(j):
             bank = psum.tile([P, 2, 2, P], F32, name="q_bank", tag="inputs")
@@ -153,13 +155,14 @@ def tile_pgwcrossattention_pa_t_kernel(tc, q, k, v_ret, pi_star, Wv, bv, gamma, 
 
         def scores(i, half):
             z[i, half] = psum.tile([P, BANK], F32, name="z", bufs=3)
+            keys = k_t[i // NB][:] if PARTED[i // NB] else k_t[i // NB][:].bitcast(BF16).rearrange("p u (k y) -> p u y k", y=2)
             for u in range(2):
                 rows = q_t[i // 2][:, i % 2, u, :].bitcast(BF16).rearrange("p (r y) -> p r y", y=2)
                 for y in range(2):
                     nc.tensor.matmul(
                         out=z[i, half][:],
                         lhsT=rows[:, :, y],
-                        rhs=k_t[i // NB][:, u, y, BANK * half : BANK * (half + 1)],
+                        rhs=keys[:, u, y, BANK * half : BANK * (half + 1)],
                         start=(u == 0 and y == 0),
                         stop=(u == 1 and y == 1),
                     )
@@ -349,12 +352,12 @@ def tile_pgwcrossattention_pa_t_kernel(tc, q, k, v_ret, pi_star, Wv, bv, gamma, 
         copy_queries(0, nc.vector.tensor_copy)
         log_stage(0)
         transpose_keys(0, 1)
-        copy_keys(0, 1, nc.scalar.copy)
+        copy_keys(0, 1, nc.vector.tensor_copy)
         log_stage(1)
         transpose_keys(0, 2)
-        copy_keys(0, 2, nc.scalar.copy)
+        copy_keys(0, 2, nc.vector.tensor_copy)
         transpose_keys(0, 3)
-        copy_keys(0, 3, nc.vector.tensor_copy)
+        copy_keys(0, 3, nc.scalar.copy)
         nc.vector.tensor_scalar(out=neg_gain[:], in0=gamma_bf[:], scalar1=-math.sqrt(H), scalar2=None, op0=ALU.mult)
 
         for h in range(TILES + 1):
@@ -362,71 +365,76 @@ def tile_pgwcrossattention_pa_t_kernel(tc, q, k, v_ret, pi_star, Wv, bv, gamma, 
             cur, mul, div, following = tick, tick - MX_LAG, tick - MX_LAG - 1, tick + 1
             exps = range(exps_until(h - 1), exps_until(h))
             logs = range(max(2, logs_until(h - 1)), logs_until(h))
-            if h < TILES:
-                scores(h, 0)
-            n, r = divmod(h - 1 - KEYS_TICK, KEYS_STEP)
-            if r == 0 and 0 <= n < 4:
-                copy_keys(1, n, nc.scalar.copy)
             if div >= 0:
                 normalise_and_store(div, False)
-            n, r = divmod(h - KEYS_TICK, KEYS_STEP)
-            if r == 0 and 0 <= n < 4:
-                transpose_keys(1, n)
-            if cur >= 0:
-                regroup_probs(cur, nc.scalar.copy)
-            if h >= 1:
-                add_prior(h - 1)
-            if cur >= 0:
-                invert_sum(cur)
             for b in range(B):
                 for c in range(2):
                     if h == value_tick(b, 4 * c + 3) + 2:
                         quantise_values(b, c)
+            if h < TILES:
+                scores(h, 0)
             for i in logs:
                 floor_stage(i)
-            for i in logs[:1]:
-                log_stage(i)
+            if h >= 1:
+                add_prior(h - 1)
             if mul >= 0:
                 weighted_values(mul)
-            if h in WEIGHT_TICK:
-                group_weights(WEIGHT_TICK.index(h))
-            if h - 1 in WEIGHT_TICK:
-                quantise_weights(WEIGHT_TICK.index(h - 1))
-            for b in range(B):
-                n = h - 2 - FEATURES_TICK[b]
-                if n % 2 == 1 and 0 <= n < 8:
-                    quantise_features(b, n // 2)
             for b in range(B):
                 for n in range(8):
                     if h == value_tick(b, n) + 1:
                         add_bias(b, n)
+            for i in exps[:1]:
+                scale_minimum(i)
+                exp_stage(i)
+            if h in WEIGHT_TICK:
+                group_weights(WEIGHT_TICK.index(h))
+            for b in range(B):
+                n = h - 2 - FEATURES_TICK[b]
+                if n % 2 == 1 and 0 <= n < 8:
+                    quantise_features(b, n // 2)
             if h < TILES:
                 scores(h, 1)
-            if h % 2 == 1 and (h + 1) // 2 < NB:
-                copy_queries((h + 1) // 2, nc.vector.tensor_copy if h < LEAD else nc.scalar.copy)
+            if h - 1 in WEIGHT_TICK:
+                quantise_weights(WEIGHT_TICK.index(h - 1))
             for b in range(B):
                 for n in range(8):
                     if h == value_tick(b, n):
                         project_values(b, n, "mx")
-            for i in logs[1:]:
+            if cur >= 0:
+                regroup_probs(cur, nc.scalar.copy)
+            n, r = divmod(h - 1 - KEYS_TICK, KEYS_STEP)
+            if r == 0 and 0 <= n < 4:
+                copy_keys(1, n, nc.scalar.copy)
+            for i in logs[:1]:
                 log_stage(i)
-            for i in exps[:1]:
-                scale_minimum(i)
-                exp_stage(i)
             for b in range(B):
                 n = h - 1 - FEATURES_TICK[b]
                 if 0 <= n < 8:
                     copy_features(b, n, nc.vector.tensor_copy if b == 1 and n % 2 == 0 else nc.scalar.copy)
+            if h % 2 == 1 and (h + 1) // 2 < NB:
+                copy_queries((h + 1) // 2, nc.vector.tensor_copy if h < LEAD else nc.scalar.copy)
+            for i in logs[1:]:
+                log_stage(i)
+            for i in exps[1:]:
+                scale_minimum(i)
+                exp_stage(i)
             if following >= 0:
                 transpose_probs(following)
+            if h >= 1:
+                row_minimum(h - 1)
+            if cur - QLAG >= 0:
+                quantise_probs(cur - QLAG)
+            n, r = divmod(h - KEYS_TICK, KEYS_STEP)
+            if r == 0 and 0 <= n < 4:
+                transpose_keys(1, n)
             if h % 2 == 0 and h // 2 + 1 < NB:
                 transpose_queries(h // 2 + 1)
+            if cur >= 0:
+                invert_sum(cur)
             for b in range(B):
                 n = h - FEATURES_TICK[b]
                 if 0 <= n < 8:
                     transpose_features(b, n, "inputs" if b else "mx")
-            if h >= 1:
-                row_minimum(h - 1)
             while loaded < min(NB, logs_until(h) // 2 + 3):
                 load_pi(loaded)
                 loaded += 1
@@ -442,11 +450,6 @@ def tile_pgwcrossattention_pa_t_kernel(tc, q, k, v_ret, pi_star, Wv, bv, gamma, 
                     load_vr(b, n // 2)
             if h + 3 - KEYS_TICK in (0, 1):
                 load_k(1, h + 3 - KEYS_TICK)
-            if cur >= 0:
-                quantise_probs(cur)
-            for i in exps[1:]:
-                scale_minimum(i)
-                exp_stage(i)
 
         first = TILES - LEAD + 1
         for i in range(exps_until(TILES), TILES):
@@ -455,6 +458,8 @@ def tile_pgwcrossattention_pa_t_kernel(tc, q, k, v_ret, pi_star, Wv, bv, gamma, 
         groups = [[first]] + [list(range(i, min(i + GROUP, TILES))) for i in range(first + 1, TILES, GROUP)]
         waiting = list(range(first - MX_LAG, first))
         divided = first - MX_LAG - 1
+        for i in range(first - QLAG, first):
+            quantise_probs(i)
         for n in range(len(groups) + 1):
             current = groups[n] if n < len(groups) else []
             for i in current:

@@ -28,14 +28,15 @@ BANK = 512
 
 LEAD = 15
 LOG_TICKS = 14
-WLOAD = (0, 4)
-WEIGHT_TICK = (2, 6)
-FEATURES_TICK = (2, 14)
-VALUES_TICK = (7, 19)
+WLOAD = (0, 2)
+WEIGHT_TICK = (2, 4)
+FEATURES_TICK = (2, 13)
+VALUES_TICK = (7, 21)
 VALUES_STEP = (1, 1)
 KEYS_TICK = 3
 KEYS_STEP = 2
-EXP_RATE = (7, 4)
+QUERIES_TICK = 14
+EXP_RATE = (8, 5)
 LAST_OWN = TILES - LEAD + 2
 MX_LAG = 1
 GROUP = 2
@@ -357,7 +358,7 @@ def tile_pgwcrossattention_pa_t_kernel(tc, q, k, v_ret, pi_star, Wv, bv, gamma, 
         transpose_keys(0, 2)
         copy_keys(0, 2, nc.vector.tensor_copy)
         transpose_keys(0, 3)
-        copy_keys(0, 3, nc.scalar.copy)
+        copy_keys(0, 3, nc.vector.tensor_copy)
         nc.vector.tensor_scalar(out=neg_gain[:], in0=gamma_bf[:], scalar1=-math.sqrt(H), scalar2=None, op0=ALU.mult)
 
         for h in range(TILES + 1):
@@ -365,76 +366,64 @@ def tile_pgwcrossattention_pa_t_kernel(tc, q, k, v_ret, pi_star, Wv, bv, gamma, 
             cur, mul, div, following = tick, tick - MX_LAG, tick - MX_LAG - 1, tick + 1
             exps = range(exps_until(h - 1), exps_until(h))
             logs = range(max(2, logs_until(h - 1)), logs_until(h))
-            if div >= 0:
-                normalise_and_store(div, False)
+            for i in logs:
+                floor_stage(i)
             for b in range(B):
                 for c in range(2):
                     if h == value_tick(b, 4 * c + 3) + 2:
                         quantise_values(b, c)
-            if h < TILES:
-                scores(h, 0)
-            for i in logs:
-                floor_stage(i)
-            if h >= 1:
-                add_prior(h - 1)
-            if mul >= 0:
-                weighted_values(mul)
             for b in range(B):
                 for n in range(8):
                     if h == value_tick(b, n) + 1:
                         add_bias(b, n)
-            for i in exps[:1]:
-                scale_minimum(i)
-                exp_stage(i)
+            if h >= 1:
+                add_prior(h - 1)
             if h in WEIGHT_TICK:
                 group_weights(WEIGHT_TICK.index(h))
+            if h < TILES:
+                scores(h, 0)
             for b in range(B):
                 n = h - 2 - FEATURES_TICK[b]
                 if n % 2 == 1 and 0 <= n < 8:
                     quantise_features(b, n // 2)
-            if h < TILES:
-                scores(h, 1)
-            if h - 1 in WEIGHT_TICK:
-                quantise_weights(WEIGHT_TICK.index(h - 1))
+            if div >= 0:
+                normalise_and_store(div, False)
+            for i in exps[:1]:
+                scale_minimum(i)
+                exp_stage(i)
+            if mul >= 0:
+                weighted_values(mul)
+            for i in logs[:1]:
+                log_stage(i)
+            n, r = divmod(h - KEYS_TICK, KEYS_STEP)
+            if r == 0 and 0 <= n < 4:
+                transpose_keys(1, n)
             for b in range(B):
                 for n in range(8):
                     if h == value_tick(b, n):
                         project_values(b, n, "mx")
             if cur >= 0:
                 regroup_probs(cur, nc.scalar.copy)
-            n, r = divmod(h - 1 - KEYS_TICK, KEYS_STEP)
-            if r == 0 and 0 <= n < 4:
-                copy_keys(1, n, nc.scalar.copy)
-            for i in logs[:1]:
-                log_stage(i)
+            if h < TILES:
+                scores(h, 1)
+            if following >= 0:
+                transpose_probs(following)
+            if h % 2 == 1 and (h + 1) // 2 < NB:
+                copy_queries((h + 1) // 2, nc.vector.tensor_copy if h < QUERIES_TICK else nc.scalar.copy)
             for b in range(B):
                 n = h - 1 - FEATURES_TICK[b]
                 if 0 <= n < 8:
                     copy_features(b, n, nc.vector.tensor_copy if b == 1 and n % 2 == 0 else nc.scalar.copy)
-            if h % 2 == 1 and (h + 1) // 2 < NB:
-                copy_queries((h + 1) // 2, nc.vector.tensor_copy if h < LEAD else nc.scalar.copy)
-            for i in logs[1:]:
-                log_stage(i)
-            for i in exps[1:]:
-                scale_minimum(i)
-                exp_stage(i)
-            if following >= 0:
-                transpose_probs(following)
-            if h >= 1:
-                row_minimum(h - 1)
-            if cur - QLAG >= 0:
-                quantise_probs(cur - QLAG)
-            n, r = divmod(h - KEYS_TICK, KEYS_STEP)
-            if r == 0 and 0 <= n < 4:
-                transpose_keys(1, n)
-            if h % 2 == 0 and h // 2 + 1 < NB:
-                transpose_queries(h // 2 + 1)
-            if cur >= 0:
-                invert_sum(cur)
             for b in range(B):
                 n = h - FEATURES_TICK[b]
                 if 0 <= n < 8:
                     transpose_features(b, n, "inputs" if b else "mx")
+            if h >= 1:
+                row_minimum(h - 1)
+            for i in logs[1:]:
+                log_stage(i)
+            if cur - QLAG >= 0:
+                quantise_probs(cur - QLAG)
             while loaded < min(NB, logs_until(h) // 2 + 3):
                 load_pi(loaded)
                 loaded += 1
@@ -450,6 +439,18 @@ def tile_pgwcrossattention_pa_t_kernel(tc, q, k, v_ret, pi_star, Wv, bv, gamma, 
                     load_vr(b, n // 2)
             if h + 3 - KEYS_TICK in (0, 1):
                 load_k(1, h + 3 - KEYS_TICK)
+            if h - 1 in WEIGHT_TICK:
+                quantise_weights(WEIGHT_TICK.index(h - 1))
+            if cur >= 0:
+                invert_sum(cur)
+            for i in exps[1:]:
+                scale_minimum(i)
+                exp_stage(i)
+            if h % 2 == 0 and h // 2 + 1 < NB:
+                transpose_queries(h // 2 + 1)
+            n, r = divmod(h - 1 - KEYS_TICK, KEYS_STEP)
+            if r == 0 and 0 <= n < 4:
+                copy_keys(1, n, nc.scalar.copy)
 
         first = TILES - LEAD + 1
         for i in range(exps_until(TILES), TILES):

import math
from contextlib import ExitStack

import concourse.mybir as mybir
from concourse.masks import make_identity

F32 = mybir.dt.float32
BF16 = mybir.dt.bfloat16
U32 = mybir.dt.uint32
U8 = mybir.dt.uint8
FP8X4 = mybir.dt.float8_e4m3fn_x4
ALU = mybir.AluOpType
ACT = mybir.ActivationFunctionType
AX = mybir.AxisListType

P = 128
PACK = 4
B, LQ, LK, DIN, H = 2, 2048, 1024, 1024, 512
FLOOR = 1e-9
FLT_MAX = 3.4028234e38
FLOPS = 2 * B * (LK * DIN * H + 2 * LQ * LK * H)

NB = LQ // P
TILES = B * NB
KEY_TILES = LK // P
BANK = 512


LEAD = 15
LOG_TICKS = 14
WLOAD = (0, 2)
WEIGHT_TICK = (2, 4)
FEATURES_TICK = (2, 13)
VALUES_TICK = (7, 21)
VALUES_STEP = (1, 1)
KEYS_TICK = 3
KEYS_STEP = 2
QUERIES_TICK = 14
EXP_RATE = (8, 5)
LAST_OWN = TILES - LEAD + 2
MX_LAG = 1
GROUP = 2
OUTSTANDING = 1
PARTED = (False, True)
QLAG = 0
TAIL_MOD = 5


def tile_pgwcrossattention_pa_t_kernel(tc, q, k, v_ret, pi_star, Wv, bv, gamma, out):
    nc = tc.nc
    inv_sqrt_h = 1.0 / math.sqrt(H)
    pi_view = pi_star.rearrange("b (n p) k -> p (b n) k", p=P)
    q_view = q.rearrange("b (n p) h -> p (b n) h", p=P)
    k_view = k.rearrange("b (n p) h -> p b n h", p=P)
    vr_view = v_ret.rearrange("b (a p y) d -> p b a y d", p=P, y=2)
    out_view = out.rearrange("b (n p) h -> p (b n) h", p=P)
    wv_view = Wv.rearrange("(a p y) h -> p a (y h)", a=4, y=2)

    with ExitStack() as ctx:
        const = ctx.enter_context(tc.tile_pool(name="const", bufs=1))
        raw = ctx.enter_context(tc.tile_pool(name="raw", bufs=2))
        keep = ctx.enter_context(tc.tile_pool(name="keep", bufs=2))
        work = ctx.enter_context(tc.tile_pool(name="work", bufs=2))
        psum = ctx.enter_context(tc.psum_pool(name="psum", bufs=2))
        ctx.enter_context(tc.manual_schedule())

        ident_f32 = const.tile([P, P], F32)
        make_identity(nc, ident_f32[:])
        minus_one = const.tile([P, 2], F32)
        nc.vector.memset(minus_one[:], -1.0)
        gamma_bf = const.tile([P, 1], BF16)
        bias_bf = const.tile([P, H], BF16)
        neg_gain = const.tile([P, 1], F32)
        wv_codes = const.tile([P, 2, H], U32, align_bytes=64)
        wv_scales = const.tile([P, 2, H], U8, align_bytes=64)

        pi_raw, q_raw, k_raw, vr_raw, wv_raw = {}, {}, {}, {}, {}
        k_bank, q_bank, vr_bank, v_bank = {}, {}, {}, {}
        w, q_t, k_t, z = {}, {}, {}, {}
        e, e_t, e_grouped, e_codes, e_scales, acc = {}, {}, {}, {}, {}, {}
        w_min, exp_bias, row_sum, row_recip = {}, {}, {}, {}
        wv_grouped, vr_grouped, vr_codes, vr_scales, v_grouped, v_codes, v_scales = {}, {}, {}, {}, {}, {}, {}

        def load_pi(j):
            pi_raw[j] = raw.tile([P, 2, LK], BF16, name="pi_raw", tag="io", bufs=4)
            nc.sync.dma_start(out=pi_raw[j][:], in_=pi_view[:, 2 * j : 2 * j + 2, :])

        def load_q(j):
            q_raw[j] = raw.tile([P, 2, H], BF16, name="q_raw", bufs=2)
            nc.sync.dma_start(out=q_raw[j][:], in_=q_view[:, 2 * j : 2 * j + 2, :])

        def load_k(b, half):
            k_raw[b, half] = raw.tile([P, 4, H], BF16, name="k_raw", bufs=2)
            nc.sync.dma_start(out=k_raw[b, half][:], in_=k_view[:, b, 4 * half : 4 * half + 4, :])

        def load_two_keys(j):
            if j % 2 == 0:
                k_raw[0, j // 2] = raw.tile([P, 4, H], BF16, name="k_raw", bufs=2)
            n = 2 * (j % 2)
            nc.sync.dma_start(out=k_raw[0, j // 2][:, n : n + 2, :], in_=k_view[:, 0, 2 * j : 2 * j + 2, :])

        def load_one_pi(i):
            if i % 2 == 0:
                pi_raw[i // 2] = raw.tile([P, 2, LK], BF16, name="pi_raw", tag="io", bufs=4)
            nc.sync.dma_start(out=pi_raw[i // 2][:, i % 2, :], in_=pi_view[:, i, :])

        def load_vr(b, j):
            vr_raw[b, j] = raw.tile([P, 2, DIN], BF16, name="vr_raw", tag="wide_raw", bufs=3)
            nc.sync.dma_start(out=vr_raw[b, j][:], in_=vr_view[:, b, j, :, :])

        def load_wv(g):
            wv_raw[g] = raw.tile([P, PACK, H], BF16, name="wv_raw", tag="wide_raw", bufs=3)
            nc.sync.dma_start(
                out=wv_raw[g][:].rearrange("p (u y) h -> p u (y h)", u=2), in_=wv_view[:, 2 * g : 2 * g + 2, :]
            )

        def floor_stage(i):
            w[i] = keep.tile([P, LK], F32, name="w", tag="w", bufs=TILES + 1)
            nc.gpsimd.tensor_scalar(
                out=w[i][:], in0=pi_raw[i // 2][:, i % 2, :], scalar1=FLT_MAX, scalar2=FLOOR, op0=ALU.min, op1=ALU.max
            )

        def log_stage(i):
            nc.scalar.activation(out=w[i][:], in_=w[i][:], func=ACT.Ln)

        def transpose_keys(b, j):
            bank = psum.tile([P, 2, 2, P], F32, name="k_bank", tag="inputs")
            for u in range(2):
                for l in range(2):
                    words = k_raw[b, j // 2][:, 2 * (j % 2) + l, :].bitcast(F32)
                    nc.tensor.transpose(out=bank[:, u, l, :], in_=words[:, u * P : (u + 1) * P], identity=ident_f32[:])
            k_bank[b, j] = bank

        def copy_keys(b, j, copy):
            if j == 0:
                k_t[b] = keep.tile([P, 2, LK], F32, name="k_t") if not PARTED[b] else keep.tile([P, 2, 2, LK], BF16, name="k_t")
            if PARTED[b]:
                copy(
                    out=k_t[b][:, :, :, 2 * j * P : (2 * j + 2) * P],
                    in_=k_bank[b, j][:].rearrange("p u l k -> p u (l k)").bitcast(BF16).rearrange("p u (k y) -> p u y k", y=2),
                )
            else:
                copy(out=k_t[b][:, :, 2 * j * P : (2 * j + 2) * P], in_=k_bank[b, j][:].rearrange("p u l k -> p u (l k)"))

        def transpose_queries(j):
            bank = psum.tile([P, 2, 2, P], F32, name="q_bank", tag="inputs")
            for l in range(2):
                words = q_raw[j][:, l, :].bitcast(F32)
                for u in range(2):
                    nc.tensor.transpose(out=bank[:, l, u, :], in_=words[:, u * P : (u + 1) * P], identity=ident_f32[:])
            q_bank[j] = bank

        def copy_queries(j, copy):
            q_t[j] = work.tile([P, 2, 2, P], F32, name="q_t")
            copy(out=q_t[j][:], in_=q_bank[j][:])

        def scores(i, half):
            z[i, half] = psum.tile([P, BANK], F32, name="z", bufs=3)
            keys = k_t[i // NB][:] if PARTED[i // NB] else k_t[i // NB][:].bitcast(BF16).rearrange("p u (k y) -> p u y k", y=2)
            for u in range(2):
                rows = q_t[i // 2][:, i % 2, u, :].bitcast(BF16).rearrange("p (r y) -> p r y", y=2)
                for y in range(2):
                    nc.tensor.matmul(
                        out=z[i, half][:],
                        lhsT=rows[:, :, y],
                        rhs=keys[:, u, y, BANK * half : BANK * (half + 1)],
                        start=(u == 0 and y == 0),
                        stop=(u == 1 and y == 1),
                    )

        def add_prior(i):
            for half in range(2):
                cols = slice(BANK * half, BANK * (half + 1))
                nc.vector.scalar_tensor_tensor(
                    out=w[i][:, cols], in0=w[i][:, cols], scalar=neg_gain[:, 0:1], in1=z[i, half][:],
                    op0=ALU.mult, op1=ALU.subtract,
                )

        def row_minimum(i):
            w_min[i] = work.tile([P, 1], F32, name="w_min", bufs=LEAD + 3)
            nc.vector.tensor_reduce(out=w_min[i][:], in_=w[i][:], axis=AX.X, op=ALU.min)

        def scale_minimum(i):
            exp_bias[i] = work.tile([P, 1], F32, name="exp_bias", bufs=8)
            nc.gpsimd.tensor_scalar(
                out=exp_bias[i][:], in0=w_min[i][:], scalar1=inv_sqrt_h, scalar2=0.0, op0=ALU.mult, op1=ALU.add
            )

        def exp_stage(i):
            e[i] = keep.tile([P, LK], BF16, name="e", tag="w", bufs=TILES + 1)
            if i % 2 == 0:
                row_sum[i // 2] = work.tile([P, 2], F32, name="row_sum", bufs=8)
            nc.scalar.activation(
                out=e[i][:], in_=w[i][:], func=ACT.Exp, bias=exp_bias[i][:, 0:1], scale=-inv_sqrt_h,
                accum_out=row_sum[i // 2][:, i % 2 : i % 2 + 1],
            )

        def transpose_probs(i):
            if i >= LAST_OWN:
                e_t[i] = psum.tile([P, PACK, P], F32, name="e_t_last", tag="z", bufs=3) if i % 2 else psum.tile([P, PACK, P], F32, name="e_t_last", tag="inputs")
            else:
                e_t[i] = psum.tile([P, PACK, P], F32, name="e_t", bufs=1)
            words = e[i][:].bitcast(F32)
            for a in range(PACK):
                nc.tensor.transpose(out=e_t[i][:, a, :], in_=words[:, a * P : (a + 1) * P], identity=ident_f32[:])

        def regroup_probs(i, copy):
            e_grouped[i] = work.tile([P, 2, P, PACK], BF16, name="e_grouped", bufs=2, align_bytes=64)
            copy(out=e_grouped[i][:].bitcast(F32), in_=e_t[i][:].rearrange("p (c u) r -> p c r u", u=2))

        def quantise_probs(i):
            e_codes[i] = work.tile([P, 2 * P], U32, name="e_codes", bufs=3, align_bytes=64)
            e_scales[i] = work.tile([P, 2 * P], U8, name="e_scales", bufs=3, align_bytes=64)
            nc.vector.quantize_mx(
                out=e_codes[i][:].bitcast(FP8X4), scales=e_scales[i][:],
                in_=e_grouped[i][:].rearrange("p c r t -> p (c r t)"),
            )

        def invert_sum(i):
            if i % 2 == 0:
                row_recip[i // 2] = work.tile([P, 2], F32, name="row_recip", bufs=4)
                nc.gpsimd.tensor_tensor(out=row_recip[i // 2][:], in0=row_sum[i // 2][:], in1=minus_one[:], op=ALU.pow)

        def weighted_values(i):
            if i > LAST_OWN and i % 3 == 0:
                acc[i] = psum.tile([P, H], F32, name="acc_last", tag="e_t", bufs=1)
            else:
                acc[i] = psum.tile([P, H], F32, name="acc", tag="mx")
            for c in range(2):
                nc.tensor.matmul_mx(
                    out=acc[i][:],
                    lhsT=e_codes[i][:, c * P : (c + 1) * P].bitcast(FP8X4),
                    lhsT_scale=e_scales[i][:, c * P : (c + 1) * P],
                    rhs=v_codes[i // NB][:, c, :].bitcast(FP8X4),
                    rhs_scale=v_scales[i // NB][:, c, :],
                    start=(c == 0),
                    stop=(c == 1),
                )

        def normalise_and_store(i, on_vector):
            if i >= LAST_OWN:
                o = keep.tile([P, H], F32, name="o_last", tag="w", bufs=TILES + 1)
            else:
                o = raw.tile([P, H], F32, name="o", tag="io", bufs=4)
            if on_vector:
                nc.vector.tensor_scalar(out=o[:], in0=acc[i][:], scalar1=row_recip[i // 2][:, i % 2 : i % 2 + 1], scalar2=None, op0=ALU.mult)
            else:
                nc.scalar.activation(out=o[:], in_=acc[i][:], func=ACT.Copy, scale=row_recip[i // 2][:, i % 2 : i % 2 + 1])
            nc.sync.dma_start(out=out_view[:, i, :], in_=o[:])

        def group_weights(g):
            wv_grouped[g] = work.tile([P, H, PACK], BF16, name="wv_grouped", tag="grouped", align_bytes=64)
            nc.vector.tensor_copy(out=wv_grouped[g][:], in_=wv_raw[g][:].rearrange("p t h -> p h t"))

        def quantise_weights(g):
            nc.vector.quantize_mx(
                out=wv_codes[:, g, :].bitcast(FP8X4), scales=wv_scales[:, g, :], in_=wv_grouped[g][:].rearrange("p h t -> p (h t)")
            )

        def transpose_features(b, n, tag):
            bank = psum.tile([P, 2, 2, P], F32, name="vr_bank", tag=tag)
            words = vr_raw[b, n // 2][:, n % 2, :].bitcast(F32)
            for g in range(2):
                for u in range(2):
                    a = 2 * g + u
                    nc.tensor.transpose(out=bank[:, g, u, :], in_=words[:, a * P : (a + 1) * P], identity=ident_f32[:])
            vr_bank[b, n] = bank

        def copy_features(b, n, copy):
            if n % 2 == 0:
                vr_grouped[b, n // 2] = work.tile([P, 2, 2, P, PACK], BF16, name="vr_grouped", tag="grouped", align_bytes=64)
            copy(
                out=vr_grouped[b, n // 2][:].bitcast(F32)[:, n % 2], in_=vr_bank[b, n][:].rearrange("p g u k -> p g k u")
            )

        def quantise_features(b, j):
            if j == 0:
                vr_codes[b] = keep.tile([P, KEY_TILES, 2, P], U32, name="vr_codes", bufs=1, align_bytes=64)
                vr_scales[b] = keep.tile([P, KEY_TILES, 2, P], U8, name="vr_scales", bufs=1, align_bytes=64)
            nc.vector.quantize_mx(
                out=vr_codes[b][:, 2 * j : 2 * j + 2].rearrange("p l g k -> p (l g k)").bitcast(FP8X4),
                scales=vr_scales[b][:, 2 * j : 2 * j + 2].rearrange("p l g k -> p (l g k)"),
                in_=vr_grouped[b, j][:].rearrange("p l g k t -> p (l g k t)"),
            )

        def project_values(b, n, tag):
            c, hc = n // 4, n % 4
            cols = slice(hc * P, (hc + 1) * P)
            bank = psum.tile([P, PACK, P], F32, name="v_bank", tag=tag)
            for t in range(PACK):
                for g in range(2):
                    nc.tensor.matmul_mx(
                        out=bank[:, t, :],
                        lhsT=vr_codes[b][:, PACK * c + t, g, :].bitcast(FP8X4),
                        lhsT_scale=vr_scales[b][:, PACK * c + t, g, :],
                        rhs=wv_codes[:, g, cols].bitcast(FP8X4),
                        rhs_scale=wv_scales[:, g, cols],
                        start=(g == 0),
                        stop=(g == 1),
                    )
            v_bank[b, n] = bank

        def add_bias(b, n):
            c, hc = n // 4, n % 4
            cols = slice(hc * P, (hc + 1) * P)
            if n == 0:
                v_codes[b] = keep.tile([P, 2, H], U32, name="v_codes", align_bytes=64)
                v_scales[b] = keep.tile([P, 2, H], U8, name="v_scales", align_bytes=64)
            if hc == 0:
                v_grouped[b, c] = work.tile([P, H, PACK], BF16, name="v_grouped", tag="grouped", align_bytes=64)
            nc.vector.tensor_tensor(
                out=v_grouped[b, c][:, cols, :],
                in0=v_bank[b, n][:].rearrange("p t h -> p h t"),
                in1=bias_bf[:, cols].unsqueeze(2).to_broadcast([P, P, PACK]),
                op=ALU.add,
            )

        def quantise_values(b, c):
            nc.vector.quantize_mx(
                out=v_codes[b][:, c, :].bitcast(FP8X4), scales=v_scales[b][:, c, :],
                in_=v_grouped[b, c][:].rearrange("p h t -> p (h t)"),
            )

        def logs_until(h):
            return max(0, min(TILES, -(-TILES * (h + 1) // LOG_TICKS)))

        def value_tick(b, n):
            return VALUES_TICK[b] + n // VALUES_STEP[b]

        def exps_until(h):
            return max(0, min(TILES, h - 1, -(-EXP_RATE[0] * (h - LEAD + 2) // EXP_RATE[1])))

        warm = const.tile([P, 1], F32)
        nc.vector.memset(warm[:], 1.0)
        nc.scalar.activation(out=warm[:], in_=warm[:], func=ACT.Ln)
        load_two_keys(0)
        load_one_pi(0)
        load_q(0)
        load_two_keys(1)
        load_one_pi(1)
        load_two_keys(2)
        load_two_keys(3)
        nc.sync.dma_start(out=gamma_bf[:], in_=gamma.partition_broadcast(P))
        load_pi(1)
        load_q(1)
        load_pi(2)
        loaded = 3
        floor_stage(0)
        floor_stage(1)
        transpose_keys(0, 0)
        copy_keys(0, 0, nc.vector.tensor_copy)
        transpose_queries(0)
        copy_queries(0, nc.vector.tensor_copy)
        log_stage(0)
        transpose_keys(0, 1)
        copy_keys(0, 1, nc.vector.tensor_copy)
        log_stage(1)
        transpose_keys(0, 2)
        copy_keys(0, 2, nc.vector.tensor_copy)
        transpose_keys(0, 3)
        copy_keys(0, 3, nc.vector.tensor_copy)
        nc.vector.tensor_scalar(out=neg_gain[:], in0=gamma_bf[:], scalar1=-math.sqrt(H), scalar2=None, op0=ALU.mult)

        for h in range(TILES + 1):
            tick = h - LEAD
            cur, mul, div, following = tick, tick - MX_LAG, tick - MX_LAG - 1, tick + 1
            exps = range(exps_until(h - 1), exps_until(h))
            logs = range(max(2, logs_until(h - 1)), logs_until(h))
            for i in logs:
                floor_stage(i)
            for b in range(B):
                for c in range(2):
                    if h == value_tick(b, 4 * c + 3) + 2:
                        quantise_values(b, c)
            for b in range(B):
                for n in range(8):
                    if h == value_tick(b, n) + 1:
                        add_bias(b, n)
            if h >= 1:
                add_prior(h - 1)
            if h in WEIGHT_TICK:
                group_weights(WEIGHT_TICK.index(h))
            if h < TILES:
                scores(h, 0)
            for b in range(B):
                n = h - 2 - FEATURES_TICK[b]
                if n % 2 == 1 and 0 <= n < 8:
                    quantise_features(b, n // 2)
            if div >= 0:
                normalise_and_store(div, False)
            for i in exps[:1]:
                scale_minimum(i)
                exp_stage(i)
            if mul >= 0:
                weighted_values(mul)
            for i in logs[:1]:
                log_stage(i)
            n, r = divmod(h - KEYS_TICK, KEYS_STEP)
            if r == 0 and 0 <= n < 4:
                transpose_keys(1, n)
            for b in range(B):
                for n in range(8):
                    if h == value_tick(b, n):
                        project_values(b, n, "mx")
            if cur >= 0:
                regroup_probs(cur, nc.scalar.copy)
            if h < TILES:
                scores(h, 1)
            if following >= 0:
                transpose_probs(following)
            if h % 2 == 1 and (h + 1) // 2 < NB:
                copy_queries((h + 1) // 2, nc.vector.tensor_copy if h < QUERIES_TICK else nc.scalar.copy)
            for b in range(B):
                n = h - 1 - FEATURES_TICK[b]
                if 0 <= n < 8:
                    copy_features(b, n, nc.vector.tensor_copy if b == 1 and n % 2 == 0 else nc.scalar.copy)
            for b in range(B):
                n = h - FEATURES_TICK[b]
                if 0 <= n < 8:
                    transpose_features(b, n, "inputs" if b else "mx")
            if h >= 1:
                row_minimum(h - 1)
            for i in logs[1:]:
                log_stage(i)
            if cur - QLAG >= 0:
                quantise_probs(cur - QLAG)
            while loaded < min(NB, logs_until(h) // 2 + 3):
                load_pi(loaded)
                loaded += 1
            if h % 2 == 0 and 2 <= h // 2 + 2 < NB:
                load_q(h // 2 + 2)
            if h in WLOAD:
                load_wv(WLOAD.index(h))
            if h == WLOAD[1]:
                nc.sync.dma_start(out=bias_bf[:], in_=bv.partition_broadcast(P))
            for b in range(B):
                n = h + 2 - FEATURES_TICK[b]
                if n % 2 == 0 and 0 <= n // 2 < 4:
                    load_vr(b, n // 2)
            if h + 3 - KEYS_TICK in (0, 1):
                load_k(1, h + 3 - KEYS_TICK)
            if h - 1 in WEIGHT_TICK:
                quantise_weights(WEIGHT_TICK.index(h - 1))
            if cur >= 0:
                invert_sum(cur)
            for i in exps[1:]:
                scale_minimum(i)
                exp_stage(i)
            if h % 2 == 0 and h // 2 + 1 < NB:
                transpose_queries(h // 2 + 1)
            n, r = divmod(h - 1 - KEYS_TICK, KEYS_STEP)
            if r == 0 and 0 <= n < 4:
                copy_keys(1, n, nc.scalar.copy)

        first = TILES - LEAD + 1
        for i in range(exps_until(TILES), TILES):
            scale_minimum(i)
            exp_stage(i)
        groups = [[first]] + [list(range(i, min(i + GROUP, TILES))) for i in range(first + 1, TILES, GROUP)]
        waiting = list(range(first - MX_LAG, first))
        divided = first - MX_LAG - 1
        for i in range(first - QLAG, first):
            quantise_probs(i)
        for n in range(len(groups) + 1):
            current = groups[n] if n < len(groups) else []
            for i in current:
                regroup_probs(i, nc.scalar.copy if i % TAIL_MOD == 0 else nc.vector.tensor_copy)
                invert_sum(i)
            for i in groups[n + 1] if n + 1 < len(groups) else []:
                transpose_probs(i)
            for i in waiting:
                if i - divided > OUTSTANDING:
                    normalise_and_store(divided, False)
                    divided += 1
                weighted_values(i)
            for i in current:
                quantise_probs(i)
            while divided < (waiting[-1] if waiting else TILES):
                normalise_and_store(divided, False)
                divided += 1
            waiting = current
        normalise_and_store(TILES - 1, False)
